import numpy as np
import ml_dtypes


def mxq(x, axis, fmt="e4m3"):
    dtype, down = {"e4m3": (ml_dtypes.float8_e4m3fn, 7), "e5m2": (ml_dtypes.float8_e5m2, 14)}[fmt]
    v = np.moveaxis(np.asarray(x, np.float32).astype(ml_dtypes.bfloat16).astype(np.float64), axis, -1)
    blocks = v.reshape(v.shape[:-1] + (-1, 32))
    amax = np.abs(blocks).max(-1, keepdims=True)
    byte = np.maximum(np.where(amax > 0, np.frexp(amax)[1] - 1 + 127, 0) - down, 1)
    scale = np.exp2(byte - 127.0)
    codes = (blocks / scale).astype(np.float32).astype(dtype).astype(np.float64)
    return np.moveaxis((codes * scale).reshape(v.shape), -1, axis)


WIDE = False


def mx_kscale(k):
    if not WIDE:
        return np.ones(k)
    levels = np.array([10, -10, 5, -5, 0])
    a = np.random.permutation(np.resize(levels, k // 512 * 4)).reshape(k // 512, 4)
    idx = np.arange(k)
    return np.exp2(a[idx // 512, idx % 128 // 32])


BF16 = ml_dtypes.bfloat16


def bf(x):
    return np.asarray(x, np.float32).astype(BF16)


def f64(x):
    return np.asarray(x).astype(np.float64)


B, R, RS, RED, F1, F2, NC = 1024, 320, 60, 16, 1024, 512, 256
C = R * RED
EPS = 1e-5
SLOPE = 0.3


def bn_train(h, gamma, beta):
    mean = h.mean(axis=0)
    var = h.var(axis=0)
    return (h - mean) * (1.0 / np.sqrt(var + EPS)) * gamma + beta


def setup_inputs():
    s = mx_kscale(C)
    sr = s.reshape(R, RED)
    sig = np.exp2(np.random.uniform(-8.0, 1.0, (R, RED)))
    off = 0.7 * np.random.standard_normal((R, RED))
    return {"h_enc": bf((np.random.standard_normal((B, R, RED)) + off) * sig),
            "enc_gamma": bf((1.0 + 0.1 * np.random.standard_normal((R, RED))) * sr),
            "enc_beta": bf(0.3 * np.random.standard_normal((R, RED)) * sr),
            "w1": bf(np.random.standard_normal((F1, C)) / np.sqrt(C) / s[None, :]),
            "b1": bf(0.3 * np.random.standard_normal(F1))}


def reference(h_enc, enc_gamma, enc_beta, w1, b1):
    h = bn_train(f64(h_enc), f64(enc_gamma), f64(enc_beta))
    h = np.where(h >= 0, h, SLOPE * h)
    c = h.reshape(B, C)
    return (mxq(c, 1, "e4m3") @ mxq(f64(w1), 1, "e4m3").T) + f64(b1)

@@ -1,0 +1,199 @@
+import concourse.bass as bass
+import concourse.mybir as mybir
+import concourse.tile as tile
+from concourse.masks import make_identity
+
+F32 = mybir.dt.float32
+BF16 = mybir.dt.bfloat16
+U32 = mybir.dt.uint32
+U8 = mybir.dt.uint8
+FP8X4 = mybir.dt.float8_e4m3fn_x4
+ALU = mybir.AluOpType
+ACT = mybir.ActivationFunctionType
+
+P = 128
+B = 1024
+C = 5120
+F = 1024
+NB = B // P
+NJ = C // 256
+NG = C // 512
+EPS = 1e-5
+SLOPE = 0.3
+FLOPS = 2 * B * C * F
+
+
+def tile_roibaseline_pa_kernel(tc, h_enc, enc_gamma, enc_beta, w1, b1, out):
+    nc = tc.nc
+    h2 = h_enc.rearrange("b r o -> b (r o)")
+    with tc.tile_pool(name="const", bufs=1) as const, \
+            tc.tile_pool(name="wpool", bufs=3) as wpool, \
+            tc.tile_pool(name="gpool", bufs=2) as gpool, \
+            tc.tile_pool(name="npool", bufs=4) as npool, \
+            tc.tile_pool(name="cpool", bufs=3) as cpool, \
+            tc.tile_pool(name="opool", bufs=2) as opool, \
+            tc.psum_pool(name="psa", bufs=4) as psa, \
+            tc.psum_pool(name="psb", bufs=4) as psb:
+        ident = const.tile([P, P], F32, name="ident")
+        make_identity(nc, ident[:])
+        one = const.tile([P, 1], F32, name="one")
+        nc.vector.memset(one[:], 1.0)
+        warm = const.tile([P, 1], F32, name="warm")
+        nc.scalar.activation(out=warm[:], in_=one[:], func=ACT.Sqrt)
+        gbn = const.tile([P, 256], BF16, name="gbn")
+        nc.vector.memset(gbn[:], 0.0)
+
+        hn = []
+        for bt in range(NB):
+            t = const.tile([P, C], BF16, name="hn%d" % bt)
+            nc.sync.dma_start(out=t[:], in_=h2[bt * P:(bt + 1) * P, :])
+            hn.append(t)
+        nc.sync.dma_start(out=gbn[0:20, :], in_=enc_gamma.rearrange("(j x) o -> j (x o)", j=NJ))
+        nc.sync.dma_start(out=gbn[32:52, :], in_=enc_beta.rearrange("(j x) o -> j (x o)", j=NJ))
+        wn = {}
+
+        def load_w(g):
+            t = wpool.tile([P, NB, 512], BF16, name="wn", tag="wn")
+            nc.sync.dma_start(out=t[:], in_=w1[:, g * 512:(g + 1) * 512].rearrange("(t p) k -> p t k", p=P))
+            wn[g] = t
+
+        for g in range(3):
+            load_w(g)
+
+        wc = const.tile([P, NG, F], U32, name="wc", align_bytes=64)
+        ws = const.tile([P, NG, F], U8, name="ws", align_bytes=64)
+        st = const.tile([P, NJ, 4, 6], F32, name="st")
+        mv = const.tile([P, 2 * NJ, 2], F32, name="mv")
+        bias = const.tile([P, F], BF16, name="bias")
+
+        def stats_unit(q, jj):
+            xs = psa.tile([P, 512], F32, name="xs", tag="xa")
+            for i2 in range(2):
+                j = 2 * jj + i2
+                for bb in range(2):
+                    nc.tensor.transpose(
+                        out=xs[:, 256 * i2 + P * bb:256 * i2 + P * bb + P],
+                        in_=hn[2 * q + bb][:].bitcast(F32)[:, P * j:P * j + P],
+                        identity=ident[:])
+            xb = xs[:].bitcast(BF16)
+            for i2 in range(2):
+                nc.vector.bn_stats(out=st[:, 2 * jj + i2, q, :], in_=xb[:, 512 * i2:512 * i2 + 512])
+
+        gws = {}
+
+        def w_group(g):
+            gw = gpool.tile([P, 4 * F], BF16, name="gw", tag="gw", align_bytes=64)
+            gws[g] = gw
+            gw32 = gw[:].bitcast(F32).rearrange("p (f u) -> p f u", u=2)
+            w32 = wn[g][:].bitcast(F32)
+            for wq in range(4):
+                wt = psb.tile([P, 512], F32, name="wt", tag="xb")
+                for u in range(2):
+                    for f2 in range(2):
+                        nc.tensor.transpose(
+                            out=wt[:, 256 * u + P * f2:256 * u + P * f2 + P],
+                            in_=w32[:, 2 * wq + f2, P * u:P * u + P],
+                            identity=ident[:])
+                nc.scalar.copy(out=gw32[:, 256 * wq:256 * wq + 256, :],
+                               in_=wt[:].rearrange("p (u f) -> p f u", u=2))
+            if g + 3 < NG:
+                load_w(g + 3)
+
+        def w_quant(g):
+            nc.vector.quantize_mx(out=wc[:, g, :].bitcast(FP8X4), scales=ws[:, g, :], in_=gws[g][:])
+
+        wg_at = {}
+        for g in range(NG):
+            wg_at[16 + (12 * g) // 5] = g
+        pending = []
+        for s in range(64):
+            if s < 40:
+                stats_unit(s // 10, s % 10)
+            if len(pending) > 0 and pending[0][0] <= s:
+                w_quant(pending[0][1])
+                pending = pending[1:]
+            if s in wg_at:
+                w_group(wg_at[s])
+                pending.append((s + 2, wg_at[s]))
+        assert len(pending) == 0
+        nc.sync.dma_start(out=bias[:], in_=b1.partition_broadcast(P))
+
+        gps = psa.tile([P, 512], F32, name="gps", tag="xa")
+        nc.tensor.transpose(out=gps[:, 0:P], in_=gbn[:].bitcast(F32), identity=ident[:])
+        gbf = const.tile([P, P], F32, name="gbf")
+        nc.vector.tensor_copy(out=gbf[:], in_=gps[:].bitcast(BF16)[:, 0:P])
+        gamma = gbf[:, 0:40]
+        beta = gbf[:, 64:104]
+        for j in range(NJ):
+            for e in range(2):
+                nc.vector.bn_aggr(out=mv[:, 2 * j + e, :], in_=st[:, j, :, 3 * e:3 * e + 3])
+        mean = mv[:, :, 0]
+        var = mv[:, :, 1]
+        veps = const.tile([P, 40], F32, name="veps")
+        sd = const.tile([P, 40], F32, name="sd")
+        r0 = const.tile([P, 40], F32, name="r0")
+        vr = const.tile([P, 40], F32, name="vr")
+        s2 = const.tile([P, 40], F32, name="s2")
+        rs = const.tile([P, 40], F32, name="rs")
+        sa = const.tile([P, 40], F32, name="sa")
+        ma = const.tile([P, 40], F32, name="ma")
+        sb = const.tile([P, 40], F32, name="sb")
+        nc.vector.tensor_scalar_add(out=veps[:], in0=var, scalar1=EPS)
+        nc.scalar.activation(out=sd[:], in_=veps[:], func=ACT.Sqrt)
+        nc.vector.reciprocal(out=r0[:], in_=sd[:])
+        nc.vector.tensor_tensor(out=vr[:], in0=veps[:], in1=r0[:], op=ALU.mult)
+        nc.vector.tensor_tensor(out=s2[:], in0=vr[:], in1=sd[:], op=ALU.add)
+        nc.vector.reciprocal(out=rs[:], in_=s2[:])
+        nc.vector.scalar_tensor_tensor(out=sa[:], in0=gamma, scalar=2.0, in1=rs[:], op0=ALU.mult, op1=ALU.mult)
+        nc.vector.tensor_tensor(out=ma[:], in0=mean, in1=sa[:], op=ALU.mult)
+        nc.vector.tensor_tensor(out=sb[:], in0=beta, in1=ma[:], op=ALU.subtract)
+
+        for r in range(4):
+            acc = [[psb.tile([P, 512], F32, name="acc", tag="xb") for fh in range(2)] for bb in range(2)]
+            for gp in range(NG // 2):
+                gc = cpool.tile([P, 2048], BF16, name="gc", tag="gc", align_bytes=64)
+                cc = cpool.tile([P, 512], U32, name="cc", tag="cc", align_bytes=64)
+                cs = cpool.tile([P, 512], U8, name="cs", tag="cs", align_bytes=64)
+                xts = []
+                for gg in range(2):
+                    g = 2 * gp + gg
+                    xt = psa.tile([P, 512], F32, name="xt", tag="xa")
+                    xts.append(xt)
+                    for u in range(2):
+                        for bb in range(2):
+                            nc.tensor.transpose(
+                                out=xt[:, 256 * u + P * bb:256 * u + P * bb + P],
+                                in_=hn[2 * r + bb][:].bitcast(F32)[:, P * (2 * g + u):P * (2 * g + u) + P],
+                                identity=ident[:])
+                for gg in range(2):
+                    g = 2 * gp + gg
+                    xv = xts[gg][:].bitcast(BF16).rearrange("p (u c e) -> p u c e", u=2, e=2)
+                    nt = npool.tile([P, 4, 256], F32, name="nt", tag="nt")
+                    for u in range(2):
+                        for e in range(2):
+                            je = 2 * (2 * g + u) + e
+                            nc.scalar.activation(out=nt[:, 2 * u + e, :], in_=xv[:, u, :, e], func=ACT.Identity,
+                                                 scale=sa[:, je:je + 1], bias=sb[:, je:je + 1])
+                    nv = nt[:].rearrange("p t c -> p c t")
+                    nc.vector.scalar_tensor_tensor(
+                        out=gc[:, 1024 * gg:1024 * gg + 1024].rearrange("p (c t) -> p c t", t=4),
+                        in0=nv, scalar=SLOPE, in1=nv, op0=ALU.mult, op1=ALU.max)
+                nc.vector.quantize_mx(out=cc[:].bitcast(FP8X4), scales=cs[:], in_=gc[:])
+                for bb in range(2):
+                    for fh in range(2):
+                        for gg in range(2):
+                            g = 2 * gp + gg
+                            col = 256 * gg + P * bb
+                            nc.tensor.matmul_mx(
+                                out=acc[bb][fh][:],
+                                lhsT=cc[:, col:col + P].bitcast(FP8X4), lhsT_scale=cs[:, col:col + P],
+                                rhs=wc[:, g, 512 * fh:512 * fh + 512].bitcast(FP8X4),
+                                rhs_scale=ws[:, g, 512 * fh:512 * fh + 512],
+                                start=(g == 0), stop=(g == NG - 1))
+            for bb in range(2):
+                ob = opool.tile([P, F], F32, name="ob", tag="ob")
+                for fh in range(2):
+                    nc.vector.tensor_tensor(out=ob[:, 512 * fh:512 * fh + 512], in0=acc[bb][fh][:],
+                                            in1=bias[:, 512 * fh:512 * fh + 512], op=ALU.add)
+                row = (2 * r + bb) * P
+                nc.sync.dma_start(out=out[row:row + P, :], in_=ob[:])

@@ -1,6 +1,4 @@
-import concourse.bass as bass
 import concourse.mybir as mybir
-import concourse.tile as tile
 from concourse.masks import make_identity
 
 F32 = mybir.dt.float32
@@ -21,19 +19,22 @@ NG = C // 512
 EPS = 1e-5
 SLOPE = 0.3
 FLOPS = 2 * B * C * F
+ND = 20
 
 
 def tile_roibaseline_pa_kernel(tc, h_enc, enc_gamma, enc_beta, w1, b1, out):
     nc = tc.nc
     h2 = h_enc.rearrange("b r o -> b (r o)")
     with tc.tile_pool(name="const", bufs=1) as const, \
-            tc.tile_pool(name="wpool", bufs=3) as wpool, \
+            tc.tile_pool(name="wpool", bufs=4) as wpool, \
             tc.tile_pool(name="gpool", bufs=2) as gpool, \
+            tc.tile_pool(name="spool", bufs=2) as spool, \
             tc.tile_pool(name="npool", bufs=4) as npool, \
             tc.tile_pool(name="cpool", bufs=3) as cpool, \
-            tc.tile_pool(name="opool", bufs=2) as opool, \
+            tc.tile_pool(name="opool", bufs=3) as opool, \
             tc.psum_pool(name="psa", bufs=4) as psa, \
-            tc.psum_pool(name="psb", bufs=4) as psb:
+            tc.psum_pool(name="psb", bufs=4) as psb, \
+            tc.manual_schedule():
         ident = const.tile([P, P], F32, name="ident")
         make_identity(nc, ident[:])
         one = const.tile([P, 1], F32, name="one")
@@ -42,52 +43,80 @@ def tile_roibaseline_pa_kernel(tc, h_enc, enc_gamma, enc_beta, w1, b1, out):
         nc.scalar.activation(out=warm[:], in_=one[:], func=ACT.Sqrt)
         gbn = const.tile([P, 256], BF16, name="gbn")
         nc.vector.memset(gbn[:], 0.0)
+        st = const.tile([P, NJ, 4, 8], F32, name="st")
+        nc.vector.memset(st[:], 256.0)
 
-        hn = []
-        for bt in range(NB):
-            t = const.tile([P, C], BF16, name="hn%d" % bt)
-            nc.sync.dma_start(out=t[:], in_=h2[bt * P:(bt + 1) * P, :])
-            hn.append(t)
         nc.sync.dma_start(out=gbn[0:20, :], in_=enc_gamma.rearrange("(j x) o -> j (x o)", j=NJ))
         nc.sync.dma_start(out=gbn[32:52, :], in_=enc_beta.rearrange("(j x) o -> j (x o)", j=NJ))
+        hn = [const.tile([P, C], BF16, name="hn%d" % bt) for bt in range(NB)]
+        for ch in range(5):
+            for bt in range(2):
+                nc.sync.dma_start(out=hn[bt][:, 1024 * ch:1024 * ch + 1024],
+                                  in_=h2[bt * P:(bt + 1) * P, 1024 * ch:1024 * ch + 1024])
+        for bt in range(2, NB):
+            nc.sync.dma_start(out=hn[bt][:], in_=h2[bt * P:(bt + 1) * P, :])
         wn = {}
 
         def load_w(g):
-            t = wpool.tile([P, NB, 512], BF16, name="wn", tag="wn")
-            nc.sync.dma_start(out=t[:], in_=w1[:, g * 512:(g + 1) * 512].rearrange("(t p) k -> p t k", p=P))
-            wn[g] = t
+            wn[g] = wpool.tile([P, NB, 512], BF16, name="wn", tag="wn")
+            nc.sync.dma_start(out=wn[g][:], in_=w1[:, g * 512:(g + 1) * 512].rearrange("(t p) k -> p t k", p=P))
 
-        for g in range(3):
+        for g in range(4):
             load_w(g)
 
         wc = const.tile([P, NG, F], U32, name="wc", align_bytes=64)
         ws = const.tile([P, NG, F], U8, name="ws", align_bytes=64)
-        st = const.tile([P, NJ, 4, 6], F32, name="st")
         mv = const.tile([P, 2 * NJ, 2], F32, name="mv")
         bias = const.tile([P, F], BF16, name="bias")
 
-        def stats_unit(q, jj):
-            xs = psa.tile([P, 512], F32, name="xs", tag="xa")
+        gps = psa.tile([P, 512], F32, name="gps", tag="xa")
+        nc.tensor.transpose(out=gps[:, 0:P], in_=gbn[:].bitcast(F32), identity=ident[:])
+        gbf = const.tile([P, P], F32, name="gbf")
+        nc.vector.tensor_copy(out=gbf[:], in_=gps[:].bitcast(BF16)[:, 0:P])
+        gamma = gbf[:, 0:40]
+        beta = gbf[:, 64:104]
+
+        def unit_bank(pool, tag, q, jj):
+            xs = pool.tile([P, 512], F32, name="xs", tag=tag)
             for i2 in range(2):
-                j = 2 * jj + i2
                 for bb in range(2):
+                    j = 2 * jj + i2
                     nc.tensor.transpose(
                         out=xs[:, 256 * i2 + P * bb:256 * i2 + P * bb + P],
                         in_=hn[2 * q + bb][:].bitcast(F32)[:, P * j:P * j + P],
                         identity=ident[:])
-            xb = xs[:].bitcast(BF16)
+            return xs[:].bitcast(BF16)
+
+        def v_unit(q, jj):
+            xb = unit_bank(psb, "xb", q, jj)
             for i2 in range(2):
-                nc.vector.bn_stats(out=st[:, 2 * jj + i2, q, :], in_=xb[:, 512 * i2:512 * i2 + 512])
+                nc.vector.bn_stats(out=st[:, 2 * jj + i2, q, 0:6], in_=xb[:, 512 * i2:512 * i2 + 512])
+
+        def s_unit(q, jj):
+            xv = unit_bank(psa, "xa", q, jj).rearrange("p (i c e) -> p i c e", i=2, e=2)
+            s1 = spool.tile([P, 4], F32, name="s1", tag="s1")
+            for i2 in range(2):
+                for e in range(2):
+                    junk = spool.tile([P, 256], BF16, name="junk", tag="junk")
+                    nc.scalar.activation(out=junk[:], in_=xv[:, i2, :, e], func=ACT.Identity,
+                                         accum_out=s1[:, 2 * i2 + e:2 * i2 + e + 1])
+            nc.scalar.activation(out=st[:, 2 * jj:2 * jj + 2, q, 1:5:3],
+                                 in_=s1[:].rearrange("p (i e) -> p i e", e=2), func=ACT.Copy, scale=1.0 / 256.0)
+            for i2 in range(2):
+                for e in range(2):
+                    junk = spool.tile([P, 256], BF16, name="junk", tag="junk")
+                    nc.scalar.activation(out=junk[:], in_=xv[:, i2, :, e], func=ACT.Square, scale=-1.0,
+                                         bias=st[:, 2 * jj + i2, q, 3 * e + 1:3 * e + 2],
+                                         accum_out=st[:, 2 * jj + i2, q, 3 * e + 2:3 * e + 3])
 
         gws = {}
 
         def w_group(g):
-            gw = gpool.tile([P, 4 * F], BF16, name="gw", tag="gw", align_bytes=64)
-            gws[g] = gw
-            gw32 = gw[:].bitcast(F32).rearrange("p (f u) -> p f u", u=2)
+            gws[g] = gpool.tile([P, 4 * F], BF16, name="gw", tag="gw", align_bytes=64)
+            gw32 = gws[g][:].bitcast(F32).rearrange("p (f u) -> p f u", u=2)
             w32 = wn[g][:].bitcast(F32)
             for wq in range(4):
-                wt = psb.tile([P, 512], F32, name="wt", tag="xb")
+                wt = psa.tile([P, 512], F32, name="wt", tag="xa")
                 for u in range(2):
                     for f2 in range(2):
                         nc.tensor.transpose(
@@ -96,34 +125,104 @@ def tile_roibaseline_pa_kernel(tc, h_enc, enc_gamma, enc_beta, w1, b1, out):
                             identity=ident[:])
                 nc.scalar.copy(out=gw32[:, 256 * wq:256 * wq + 256, :],
                                in_=wt[:].rearrange("p (u f) -> p f u", u=2))
-            if g + 3 < NG:
-                load_w(g + 3)
+            if g + 4 < NG:
+                load_w(g + 4)
 
         def w_quant(g):
             nc.vector.quantize_mx(out=wc[:, g, :].bitcast(FP8X4), scales=ws[:, g, :], in_=gws[g][:])
 
-        wg_at = {}
-        for g in range(NG):
-            wg_at[16 + (12 * g) // 5] = g
-        pending = []
-        for s in range(64):
-            if s < 40:
-                stats_unit(s // 10, s % 10)
-            if len(pending) > 0 and pending[0][0] <= s:
-                w_quant(pending[0][1])
-                pending = pending[1:]
-            if s in wg_at:
-                w_group(wg_at[s])
-                pending.append((s + 2, wg_at[s]))
-        assert len(pending) == 0
-        nc.sync.dma_start(out=bias[:], in_=b1.partition_broadcast(P))
+        wstate = {"g": 0}
 
-        gps = psa.tile([P, 512], F32, name="gps", tag="xa")
-        nc.tensor.transpose(out=gps[:, 0:P], in_=gbn[:].bitcast(F32), identity=ident[:])
-        gbf = const.tile([P, P], F32, name="gbf")
-        nc.vector.tensor_copy(out=gbf[:], in_=gps[:].bitcast(BF16)[:, 0:P])
-        gamma = gbf[:, 0:40]
-        beta = gbf[:, 64:104]
+        def w_slot():
+            g = wstate["g"]
+            if g < NG:
+                w_group(g)
+            if 1 <= g <= NG:
+                w_quant(g - 1)
+            wstate["g"] = g + 1
+
+        nv = 0
+        for q in range(4):
+            for half in range(2):
+                for i in range(4):
+                    v_unit(q, 4 * half + i)
+                    nv += 1
+                    if nv >= 20 and nv % 2 == 0:
+                        w_slot()
+                s_unit(q, 8 + half)
+
+        xts = {}
+        nts = {}
+        gcs = {}
+        ccs = {}
+        accs = {}
+
+        def t_step(d):
+            r, gp = d // 5, d % 5
+            for gg in range(2):
+                g = 2 * gp + gg
+                xt = psa.tile([P, 512], F32, name="xt", tag="xa")
+                xts[(d, gg)] = xt
+                for u in range(2):
+                    for bb in range(2):
+                        nc.tensor.transpose(
+                            out=xt[:, 256 * u + P * bb:256 * u + P * bb + P],
+                            in_=hn[2 * r + bb][:].bitcast(F32)[:, P * (2 * g + u):P * (2 * g + u) + P],
+                            identity=ident[:])
+
+        def a_step(d):
+            gp = d % 5
+            for gg in range(2):
+                g = 2 * gp + gg
+                xv = xts[(d, gg)][:].bitcast(BF16).rearrange("p (u c e) -> p u c e", u=2, e=2)
+                nt = npool.tile([P, 4, 256], F32, name="nt", tag="nt")
+                nts[(d, gg)] = nt
+                for u in range(2):
+                    for e in range(2):
+                        je = 2 * (2 * g + u) + e
+                        nc.scalar.activation(out=nt[:, 2 * u + e, :], in_=xv[:, u, :, e], func=ACT.Identity,
+                                             scale=sa[:, je:je + 1], bias=sb[:, je:je + 1])
+
+        def l_step(d, gg):
+            if gg == 0:
+                gcs[d] = cpool.tile([P, 2048], BF16, name="gc", tag="gc", align_bytes=64)
+            nv4 = nts[(d, gg)][:].rearrange("p t c -> p c t")
+            nc.vector.scalar_tensor_tensor(
+                out=gcs[d][:, 1024 * gg:1024 * gg + 1024].rearrange("p (c t) -> p c t", t=4),
+                in0=nv4, scalar=SLOPE, in1=nv4, op0=ALU.mult, op1=ALU.max)
+
+        def q_step(d):
+            cc = cpool.tile([P, 512], U32, name="cc", tag="cc", align_bytes=64)
+            cs = cpool.tile([P, 512], U8, name="cs", tag="cs", align_bytes=64)
+            ccs[d] = (cc, cs)
+            nc.vector.quantize_mx(out=cc[:].bitcast(FP8X4), scales=cs[:], in_=gcs[d][:])
+
+        def m_step(d):
+            r, gp = d // 5, d % 5
+            if gp == 0:
+                accs[r] = [[psb.tile([P, 512], F32, name="acc", tag="xb") for fh in range(2)] for bb in range(2)]
+            cc, cs = ccs[d]
+            for bb in range(2):
+                for fh in range(2):
+                    for gg in range(2):
+                        g = 2 * gp + gg
+                        col = 256 * gg + P * bb
+                        nc.tensor.matmul_mx(
+                            out=accs[r][bb][fh][:],
+                            lhsT=cc[:, col:col + P].bitcast(FP8X4), lhsT_scale=cs[:, col:col + P],
+                            rhs=wc[:, g, 512 * fh:512 * fh + 512].bitcast(FP8X4),
+                            rhs_scale=ws[:, g, 512 * fh:512 * fh + 512],
+                            start=(g == 0), stop=(g == NG - 1))
+
+        def e_step(r):
+            for bb in range(2):
+                for fh in range(2):
+                    ob = opool.tile([P, 512], F32, name="ob", tag="ob")
+                    nc.vector.tensor_tensor(out=ob[:], in0=accs[r][bb][fh][:],
+                                            in1=bias[:, 512 * fh:512 * fh + 512], op=ALU.add)
+                    row = (2 * r + bb) * P
+                    nc.sync.dma_start(out=out[row:row + P, 512 * fh:512 * fh + 512], in_=ob[:])
+
         for j in range(NJ):
             for e in range(2):
                 nc.vector.bn_aggr(out=mv[:, 2 * j + e, :], in_=st[:, j, :, 3 * e:3 * e + 3])
@@ -140,6 +239,8 @@ def tile_roibaseline_pa_kernel(tc, h_enc, enc_gamma, enc_beta, w1, b1, out):
         sb = const.tile([P, 40], F32, name="sb")
         nc.vector.tensor_scalar_add(out=veps[:], in0=var, scalar1=EPS)
         nc.scalar.activation(out=sd[:], in_=veps[:], func=ACT.Sqrt)
+        w_slot()
+        t_step(0)
         nc.vector.reciprocal(out=r0[:], in_=sd[:])
         nc.vector.tensor_tensor(out=vr[:], in0=veps[:], in1=r0[:], op=ALU.mult)
         nc.vector.tensor_tensor(out=s2[:], in0=vr[:], in1=sd[:], op=ALU.add)
@@ -147,53 +248,22 @@ def tile_roibaseline_pa_kernel(tc, h_enc, enc_gamma, enc_beta, w1, b1, out):
         nc.vector.scalar_tensor_tensor(out=sa[:], in0=gamma, scalar=2.0, in1=rs[:], op0=ALU.mult, op1=ALU.mult)
         nc.vector.tensor_tensor(out=ma[:], in0=mean, in1=sa[:], op=ALU.mult)
         nc.vector.tensor_tensor(out=sb[:], in0=beta, in1=ma[:], op=ALU.subtract)
+        nc.sync.dma_start(out=bias[:], in_=b1.partition_broadcast(P))
 
-        for r in range(4):
-            acc = [[psb.tile([P, 512], F32, name="acc", tag="xb") for fh in range(2)] for bb in range(2)]
-            for gp in range(NG // 2):
-                gc = cpool.tile([P, 2048], BF16, name="gc", tag="gc", align_bytes=64)
-                cc = cpool.tile([P, 512], U32, name="cc", tag="cc", align_bytes=64)
-                cs = cpool.tile([P, 512], U8, name="cs", tag="cs", align_bytes=64)
-                xts = []
-                for gg in range(2):
-                    g = 2 * gp + gg
-                    xt = psa.tile([P, 512], F32, name="xt", tag="xa")
-                    xts.append(xt)
-                    for u in range(2):
-                        for bb in range(2):
-                            nc.tensor.transpose(
-                                out=xt[:, 256 * u + P * bb:256 * u + P * bb + P],
-                                in_=hn[2 * r + bb][:].bitcast(F32)[:, P * (2 * g + u):P * (2 * g + u) + P],
-                                identity=ident[:])
-                for gg in range(2):
-                    g = 2 * gp + gg
-                    xv = xts[gg][:].bitcast(BF16).rearrange("p (u c e) -> p u c e", u=2, e=2)
-                    nt = npool.tile([P, 4, 256], F32, name="nt", tag="nt")
-                    for u in range(2):
-                        for e in range(2):
-                            je = 2 * (2 * g + u) + e
-                            nc.scalar.activation(out=nt[:, 2 * u + e, :], in_=xv[:, u, :, e], func=ACT.Identity,
-                                                 scale=sa[:, je:je + 1], bias=sb[:, je:je + 1])
-                    nv = nt[:].rearrange("p t c -> p c t")
-                    nc.vector.scalar_tensor_tensor(
-                        out=gc[:, 1024 * gg:1024 * gg + 1024].rearrange("p (c t) -> p c t", t=4),
-                        in0=nv, scalar=SLOPE, in1=nv, op0=ALU.mult, op1=ALU.max)
-                nc.vector.quantize_mx(out=cc[:].bitcast(FP8X4), scales=cs[:], in_=gc[:])
-                for bb in range(2):
-                    for fh in range(2):
-                        for gg in range(2):
-                            g = 2 * gp + gg
-                            col = 256 * gg + P * bb
-                            nc.tensor.matmul_mx(
-                                out=acc[bb][fh][:],
-                                lhsT=cc[:, col:col + P].bitcast(FP8X4), lhsT_scale=cs[:, col:col + P],
-                                rhs=wc[:, g, 512 * fh:512 * fh + 512].bitcast(FP8X4),
-                                rhs_scale=ws[:, g, 512 * fh:512 * fh + 512],
-                                start=(g == 0), stop=(g == NG - 1))
-            for bb in range(2):
-                ob = opool.tile([P, F], F32, name="ob", tag="ob")
-                for fh in range(2):
-                    nc.vector.tensor_tensor(out=ob[:, 512 * fh:512 * fh + 512], in0=acc[bb][fh][:],
-                                            in1=bias[:, 512 * fh:512 * fh + 512], op=ALU.add)
-                row = (2 * r + bb) * P
-                nc.sync.dma_start(out=out[row:row + P, :], in_=ob[:])
+        for p in range(ND + 3):
+            if p < ND:
+                a_step(p)
+            if p < 3:
+                w_slot()
+            if p + 1 < ND:
+                t_step(p + 1)
+            if 1 <= p <= ND:
+                l_step(p - 1, 0)
+            if p >= 7 and (p - 7) % 5 == 0:
+                e_step((p - 7) // 5)
+            if 2 <= p <= ND + 1:
+                q_step(p - 2)
+            if 1 <= p <= ND:
+                l_step(p - 1, 1)
+            if 2 <= p <= ND + 1:
+                m_step(p - 2)

@@ -26,7 +26,7 @@ def tile_roibaseline_pa_kernel(tc, h_enc, enc_gamma, enc_beta, w1, b1, out):
     nc = tc.nc
     h2 = h_enc.rearrange("b r o -> b (r o)")
     with tc.tile_pool(name="const", bufs=1) as const, \
-            tc.tile_pool(name="wpool", bufs=4) as wpool, \
+            tc.tile_pool(name="wpool", bufs=3) as wpool, \
             tc.tile_pool(name="gpool", bufs=2) as gpool, \
             tc.tile_pool(name="spool", bufs=2) as spool, \
             tc.tile_pool(name="npool", bufs=4) as npool, \
@@ -61,7 +61,7 @@ def tile_roibaseline_pa_kernel(tc, h_enc, enc_gamma, enc_beta, w1, b1, out):
             wn[g] = wpool.tile([P, NB, 512], BF16, name="wn", tag="wn")
             nc.sync.dma_start(out=wn[g][:], in_=w1[:, g * 512:(g + 1) * 512].rearrange("(t p) k -> p t k", p=P))
 
-        for g in range(4):
+        for g in range(3):
             load_w(g)
 
         wc = const.tile([P, NG, F], U32, name="wc", align_bytes=64)
@@ -125,8 +125,8 @@ def tile_roibaseline_pa_kernel(tc, h_enc, enc_gamma, enc_beta, w1, b1, out):
                             identity=ident[:])
                 nc.scalar.copy(out=gw32[:, 256 * wq:256 * wq + 256, :],
                                in_=wt[:].rearrange("p (u f) -> p f u", u=2))
-            if g + 4 < NG:
-                load_w(g + 4)
+            if g + 3 < NG:
+                load_w(g + 3)
 
         def w_quant(g):
             nc.vector.quantize_mx(out=wc[:, g, :].bitcast(FP8X4), scales=ws[:, g, :], in_=gws[g][:])
@@ -154,6 +154,7 @@ def tile_roibaseline_pa_kernel(tc, h_enc, enc_gamma, enc_beta, w1, b1, out):
         xts = {}
         nts = {}
         gcs = {}
+        cps = {}
         ccs = {}
         accs = {}
 
@@ -186,10 +187,16 @@ def tile_roibaseline_pa_kernel(tc, h_enc, enc_gamma, enc_beta, w1, b1, out):
         def l_step(d, gg):
             if gg == 0:
                 gcs[d] = cpool.tile([P, 2048], BF16, name="gc", tag="gc", align_bytes=64)
-            nv4 = nts[(d, gg)][:].rearrange("p t c -> p c t")
+            nfl = nts[(d, gg)][:].rearrange("p t c -> p (t c)")
+            cps[(d, gg)] = cpool.tile([P, 4, 256], BF16, name="cp", tag="cp")
             nc.vector.scalar_tensor_tensor(
-                out=gcs[d][:, 1024 * gg:1024 * gg + 1024].rearrange("p (c t) -> p c t", t=4),
-                in0=nv4, scalar=SLOPE, in1=nv4, op0=ALU.mult, op1=ALU.max)
+                out=cps[(d, gg)][:].rearrange("p t c -> p (t c)"),
+                in0=nfl, scalar=SLOPE, in1=nfl, op0=ALU.mult, op1=ALU.max)
+
+        def r_step(d, gg):
+            nc.vector.tensor_copy(
+                out=gcs[d][:, 1024 * gg:1024 * gg + 1024].rearrange("p (c i t) -> p c t i", i=4, t=4),
+                in_=cps[(d, gg)][:].rearrange("p t (c i) -> p c t i", i=4))
 
         def q_step(d):
             cc = cpool.tile([P, 512], U32, name="cc", tag="cc", align_bytes=64)
@@ -265,5 +272,7 @@ def tile_roibaseline_pa_kernel(tc, h_enc, enc_gamma, enc_beta, w1, b1, out):
                 q_step(p - 2)
             if 1 <= p <= ND:
                 l_step(p - 1, 1)
+                r_step(p - 1, 0)
+                r_step(p - 1, 1)
             if 2 <= p <= ND + 1:
                 m_step(p - 2)

@@ -26,7 +26,7 @@ def tile_roibaseline_pa_kernel(tc, h_enc, enc_gamma, enc_beta, w1, b1, out):
     nc = tc.nc
     h2 = h_enc.rearrange("b r o -> b (r o)")
     with tc.tile_pool(name="const", bufs=1) as const, \
-            tc.tile_pool(name="wpool", bufs=3) as wpool, \
+            tc.tile_pool(name="wpool", bufs=4) as wpool, \
             tc.tile_pool(name="gpool", bufs=2) as gpool, \
             tc.tile_pool(name="spool", bufs=2) as spool, \
             tc.tile_pool(name="npool", bufs=4) as npool, \
@@ -61,7 +61,7 @@ def tile_roibaseline_pa_kernel(tc, h_enc, enc_gamma, enc_beta, w1, b1, out):
             wn[g] = wpool.tile([P, NB, 512], BF16, name="wn", tag="wn")
             nc.sync.dma_start(out=wn[g][:], in_=w1[:, g * 512:(g + 1) * 512].rearrange("(t p) k -> p t k", p=P))
 
-        for g in range(3):
+        for g in range(4):
             load_w(g)
 
         wc = const.tile([P, NG, F], U32, name="wc", align_bytes=64)
@@ -125,8 +125,8 @@ def tile_roibaseline_pa_kernel(tc, h_enc, enc_gamma, enc_beta, w1, b1, out):
                             identity=ident[:])
                 nc.scalar.copy(out=gw32[:, 256 * wq:256 * wq + 256, :],
                                in_=wt[:].rearrange("p (u f) -> p f u", u=2))
-            if g + 3 < NG:
-                load_w(g + 3)
+            if g + 4 < NG:
+                load_w(g + 4)
 
         def w_quant(g):
             nc.vector.quantize_mx(out=wc[:, g, :].bitcast(FP8X4), scales=ws[:, g, :], in_=gws[g][:])
@@ -154,7 +154,6 @@ def tile_roibaseline_pa_kernel(tc, h_enc, enc_gamma, enc_beta, w1, b1, out):
         xts = {}
         nts = {}
         gcs = {}
-        cps = {}
         ccs = {}
         accs = {}
 
@@ -181,22 +180,21 @@ def tile_roibaseline_pa_kernel(tc, h_enc, enc_gamma, enc_beta, w1, b1, out):
                 for u in range(2):
                     for e in range(2):
                         je = 2 * (2 * g + u) + e
-                        nc.scalar.activation(out=nt[:, 2 * u + e, :], in_=xv[:, u, :, e], func=ACT.Identity,
-                                             scale=sa[:, je:je + 1], bias=sb[:, je:je + 1])
+                        if gg == 1 and d % 2 == 1:
+                            nc.vector.tensor_scalar(out=nt[:, 2 * u + e, :], in0=xv[:, u, :, e],
+                                                    scalar1=sa[:, je:je + 1], scalar2=sb[:, je:je + 1],
+                                                    op0=ALU.mult, op1=ALU.add)
+                        else:
+                            nc.scalar.activation(out=nt[:, 2 * u + e, :], in_=xv[:, u, :, e], func=ACT.Identity,
+                                                 scale=sa[:, je:je + 1], bias=sb[:, je:je + 1])
 
         def l_step(d, gg):
             if gg == 0:
                 gcs[d] = cpool.tile([P, 2048], BF16, name="gc", tag="gc", align_bytes=64)
-            nfl = nts[(d, gg)][:].rearrange("p t c -> p (t c)")
-            cps[(d, gg)] = cpool.tile([P, 4, 256], BF16, name="cp", tag="cp")
+            nv4 = nts[(d, gg)][:].rearrange("p t c -> p c t")
             nc.vector.scalar_tensor_tensor(
-                out=cps[(d, gg)][:].rearrange("p t c -> p (t c)"),
-                in0=nfl, scalar=SLOPE, in1=nfl, op0=ALU.mult, op1=ALU.max)
-
-        def r_step(d, gg):
-            nc.vector.tensor_copy(
-                out=gcs[d][:, 1024 * gg:1024 * gg + 1024].rearrange("p (c i t) -> p c t i", i=4, t=4),
-                in_=cps[(d, gg)][:].rearrange("p t (c i) -> p c t i", i=4))
+                out=gcs[d][:, 1024 * gg:1024 * gg + 1024].rearrange("p (c t) -> p c t", t=4),
+                in0=nv4, scalar=SLOPE, in1=nv4, op0=ALU.mult, op1=ALU.max)
 
         def q_step(d):
             cc = cpool.tile([P, 512], U32, name="cc", tag="cc", align_bytes=64)
@@ -272,7 +270,5 @@ def tile_roibaseline_pa_kernel(tc, h_enc, enc_gamma, enc_beta, w1, b1, out):
                 q_step(p - 2)
             if 1 <= p <= ND:
                 l_step(p - 1, 1)
-                r_step(p - 1, 0)
-                r_step(p - 1, 1)
             if 2 <= p <= ND + 1:
                 m_step(p - 2)

@@ -49,7 +49,7 @@ def tile_roibaseline_pa_kernel(tc, h_enc, enc_gamma, enc_beta, w1, b1, out):
         nc.sync.dma_start(out=gbn[0:20, :], in_=enc_gamma.rearrange("(j x) o -> j (x o)", j=NJ))
         nc.sync.dma_start(out=gbn[32:52, :], in_=enc_beta.rearrange("(j x) o -> j (x o)", j=NJ))
         hn = [const.tile([P, C], BF16, name="hn%d" % bt) for bt in range(NB)]
-        for ch in range(5):
+        for ch in (0, 4, 1, 2, 3):
             for bt in range(2):
                 nc.sync.dma_start(out=hn[bt][:, 1024 * ch:1024 * ch + 1024],
                                   in_=h2[bt * P:(bt + 1) * P, 1024 * ch:1024 * ch + 1024])
@@ -66,7 +66,6 @@ def tile_roibaseline_pa_kernel(tc, h_enc, enc_gamma, enc_beta, w1, b1, out):
 
         wc = const.tile([P, NG, F], U32, name="wc", align_bytes=64)
         ws = const.tile([P, NG, F], U8, name="ws", align_bytes=64)
-        mv = const.tile([P, 2 * NJ, 2], F32, name="mv")
         bias = const.tile([P, F], BF16, name="bias")
 
         gps = psa.tile([P, 512], F32, name="gps", tag="xa")
@@ -133,23 +132,26 @@ def tile_roibaseline_pa_kernel(tc, h_enc, enc_gamma, enc_beta, w1, b1, out):
 
         wstate = {"g": 0}
 
-        def w_slot():
-            g = wstate["g"]
-            if g < NG:
-                w_group(g)
-            if 1 <= g <= NG:
-                w_quant(g - 1)
-            wstate["g"] = g + 1
+        def w_slot_group():
+            if wstate["g"] < NG:
+                w_group(wstate["g"])
+
+        def w_slot_quant():
+            if 1 <= wstate["g"] <= NG:
+                w_quant(wstate["g"] - 1)
+            wstate["g"] = wstate["g"] + 1
 
         nv = 0
         for q in range(4):
-            for half in range(2):
-                for i in range(4):
-                    v_unit(q, 4 * half + i)
-                    nv += 1
-                    if nv >= 20 and nv % 2 == 0:
-                        w_slot()
-                s_unit(q, 8 + half)
+            for i in range(8):
+                if i == (2 if q == 0 else 0):
+                    s_unit(q, 8)
+                    s_unit(q, 9)
+                v_unit(q, i)
+                nv += 1
+                if nv >= 28 and nv % 2 == 0:
+                    w_slot_group()
+                    w_slot_quant()
 
         xts = {}
         nts = {}
@@ -180,13 +182,8 @@ def tile_roibaseline_pa_kernel(tc, h_enc, enc_gamma, enc_beta, w1, b1, out):
                 for u in range(2):
                     for e in range(2):
                         je = 2 * (2 * g + u) + e
-                        if gg == 1 and d % 2 == 1:
-                            nc.vector.tensor_scalar(out=nt[:, 2 * u + e, :], in0=xv[:, u, :, e],
-                                                    scalar1=sa[:, je:je + 1], scalar2=sb[:, je:je + 1],
-                                                    op0=ALU.mult, op1=ALU.add)
-                        else:
-                            nc.scalar.activation(out=nt[:, 2 * u + e, :], in_=xv[:, u, :, e], func=ACT.Identity,
-                                                 scale=sa[:, je:je + 1], bias=sb[:, je:je + 1])
+                        nc.scalar.activation(out=nt[:, 2 * u + e, :], in_=xv[:, u, :, e], func=ACT.Identity,
+                                             scale=sa[:, je:je + 1], bias=sb[:, je:je + 1])
 
         def l_step(d, gg):
             if gg == 0:
@@ -228,11 +225,25 @@ def tile_roibaseline_pa_kernel(tc, h_enc, enc_gamma, enc_beta, w1, b1, out):
                     row = (2 * r + bb) * P
                     nc.sync.dma_start(out=out[row:row + P, 512 * fh:512 * fh + 512], in_=ob[:])
 
-        for j in range(NJ):
-            for e in range(2):
-                nc.vector.bn_aggr(out=mv[:, 2 * j + e, :], in_=st[:, j, :, 3 * e:3 * e + 3])
-        mean = mv[:, :, 0]
-        var = mv[:, :, 1]
+        mq = st[:, :, :, 1:5:3].rearrange("p j q e -> p j e q")
+        m2q = st[:, :, :, 2:6:3].rearrange("p j q e -> p j e q")
+        msum = const.tile([P, NJ, 2], F32, name="msum")
+        mean3 = const.tile([P, NJ, 2], F32, name="mean3")
+        dq = const.tile([P, NJ, 2, 4], F32, name="dq")
+        dd = const.tile([P, NJ, 2, 4], F32, name="dd")
+        r1 = const.tile([P, NJ, 2], F32, name="r1")
+        r2 = const.tile([P, NJ, 2], F32, name="r2")
+        v1 = const.tile([P, 40], F32, name="v1")
+        nc.vector.tensor_reduce(out=msum[:], in_=mq, axis=mybir.AxisListType.X, op=ALU.add)
+        nc.vector.tensor_reduce(out=r1[:], in_=m2q, axis=mybir.AxisListType.X, op=ALU.add)
+        nc.vector.tensor_scalar_mul(out=mean3[:], in0=msum[:], scalar1=0.25)
+        nc.vector.tensor_scalar(out=v1[:], in0=r1[:].rearrange("p j e -> p (j e)"), scalar1=1.0 / B, scalar2=EPS,
+                                op0=ALU.mult, op1=ALU.add)
+        nc.vector.tensor_tensor(out=dq[:], in0=mq, in1=mean3[:].unsqueeze(3).to_broadcast([P, NJ, 2, 4]),
+                                op=ALU.subtract)
+        nc.vector.tensor_tensor(out=dd[:], in0=dq[:], in1=dq[:], op=ALU.mult)
+        nc.vector.tensor_reduce(out=r2[:], in_=dd[:], axis=mybir.AxisListType.X, op=ALU.add)
+        mean = mean3[:].rearrange("p j e -> p (j e)")
         veps = const.tile([P, 40], F32, name="veps")
         sd = const.tile([P, 40], F32, name="sd")
         r0 = const.tile([P, 40], F32, name="r0")
@@ -242,9 +253,11 @@ def tile_roibaseline_pa_kernel(tc, h_enc, enc_gamma, enc_beta, w1, b1, out):
         sa = const.tile([P, 40], F32, name="sa")
         ma = const.tile([P, 40], F32, name="ma")
         sb = const.tile([P, 40], F32, name="sb")
-        nc.vector.tensor_scalar_add(out=veps[:], in0=var, scalar1=EPS)
+        nc.vector.scalar_tensor_tensor(out=veps[:], in0=r2[:].rearrange("p j e -> p (j e)"), scalar=0.25, in1=v1[:],
+                                       op0=ALU.mult, op1=ALU.add)
         nc.scalar.activation(out=sd[:], in_=veps[:], func=ACT.Sqrt)
-        w_slot()
+        w_slot_group()
+        w_slot_quant()
         t_step(0)
         nc.vector.reciprocal(out=r0[:], in_=sd[:])
         nc.vector.tensor_tensor(out=vr[:], in0=veps[:], in1=r0[:], op=ALU.mult)
@@ -258,8 +271,7 @@ def tile_roibaseline_pa_kernel(tc, h_enc, enc_gamma, enc_beta, w1, b1, out):
         for p in range(ND + 3):
             if p < ND:
                 a_step(p)
-            if p < 3:
-                w_slot()
+            w_slot_group()
             if p + 1 < ND:
                 t_step(p + 1)
             if 1 <= p <= ND:
@@ -270,5 +282,6 @@ def tile_roibaseline_pa_kernel(tc, h_enc, enc_gamma, enc_beta, w1, b1, out):
                 q_step(p - 2)
             if 1 <= p <= ND:
                 l_step(p - 1, 1)
+            w_slot_quant()
             if 2 <= p <= ND + 1:
                 m_step(p - 2)

@@ -75,8 +75,18 @@ def tile_roibaseline_pa_kernel(tc, h_enc, enc_gamma, enc_beta, w1, b1, out):
         gamma = gbf[:, 0:40]
         beta = gbf[:, 64:104]
 
+        banks = {"n": 0}
+
+        def keep_clock(bank):
+            banks["n"] = banks["n"] + 1
+            if banks["n"] % 2 == 0 and banks["on"]:
+                nc.tensor.matmul(out=bank[:], lhsT=hn[0][:, 0:P], rhs=hn[0][:, 0:512], start=True, stop=True)
+
+        banks["on"] = True
+
         def unit_bank(pool, tag, q, jj):
             xs = pool.tile([P, 512], F32, name="xs", tag=tag)
+            keep_clock(xs)
             for i2 in range(2):
                 for bb in range(2):
                     j = 2 * jj + i2
@@ -116,6 +126,7 @@ def tile_roibaseline_pa_kernel(tc, h_enc, enc_gamma, enc_beta, w1, b1, out):
             w32 = wn[g][:].bitcast(F32)
             for wq in range(4):
                 wt = psa.tile([P, 512], F32, name="wt", tag="xa")
+                keep_clock(wt)
                 for u in range(2):
                     for f2 in range(2):
                         nc.tensor.transpose(
@@ -149,7 +160,7 @@ def tile_roibaseline_pa_kernel(tc, h_enc, enc_gamma, enc_beta, w1, b1, out):
                     s_unit(q, 9)
                 v_unit(q, i)
                 nv += 1
-                if nv >= 28 and nv % 2 == 0:
+                if nv >= 20 and nv % 2 == 0:
                     w_slot_group()
                     w_slot_quant()
 
@@ -268,6 +279,7 @@ def tile_roibaseline_pa_kernel(tc, h_enc, enc_gamma, enc_beta, w1, b1, out):
         nc.vector.tensor_tensor(out=sb[:], in0=beta, in1=ma[:], op=ALU.subtract)
         nc.sync.dma_start(out=bias[:], in_=b1.partition_broadcast(P))
 
+        banks["on"] = False
         for p in range(ND + 3):
             if p < ND:
                 a_step(p)

@@ -26,10 +26,12 @@ def tile_roibaseline_pa_kernel(tc, h_enc, enc_gamma, enc_beta, w1, b1, out):
     nc = tc.nc
     h2 = h_enc.rearrange("b r o -> b (r o)")
     with tc.tile_pool(name="const", bufs=1) as const, \
-            tc.tile_pool(name="wpool", bufs=4) as wpool, \
+            tc.tile_pool(name="big", bufs=5) as big, \
+            tc.tile_pool(name="wpool", bufs=2) as wpool, \
             tc.tile_pool(name="gpool", bufs=2) as gpool, \
             tc.tile_pool(name="spool", bufs=2) as spool, \
             tc.tile_pool(name="npool", bufs=4) as npool, \
+            tc.tile_pool(name="gcpool", bufs=2) as gcpool, \
             tc.tile_pool(name="cpool", bufs=3) as cpool, \
             tc.tile_pool(name="opool", bufs=3) as opool, \
             tc.psum_pool(name="psa", bufs=4) as psa, \
@@ -48,20 +50,21 @@ def tile_roibaseline_pa_kernel(tc, h_enc, enc_gamma, enc_beta, w1, b1, out):
 
         nc.sync.dma_start(out=gbn[0:20, :], in_=enc_gamma.rearrange("(j x) o -> j (x o)", j=NJ))
         nc.sync.dma_start(out=gbn[32:52, :], in_=enc_beta.rearrange("(j x) o -> j (x o)", j=NJ))
-        hn = [const.tile([P, C], BF16, name="hn%d" % bt) for bt in range(NB)]
+        hp = [big.tile([P, 2, C], BF16, name="hp", tag="hx") for q in range(4)]
         for ch in (0, 4, 1, 2, 3):
             for bt in range(2):
-                nc.sync.dma_start(out=hn[bt][:, 1024 * ch:1024 * ch + 1024],
+                nc.sync.dma_start(out=hp[0][:, bt, 1024 * ch:1024 * ch + 1024],
                                   in_=h2[bt * P:(bt + 1) * P, 1024 * ch:1024 * ch + 1024])
         for bt in range(2, NB):
-            nc.sync.dma_start(out=hn[bt][:], in_=h2[bt * P:(bt + 1) * P, :])
+            nc.sync.dma_start(out=hp[bt // 2][:, bt % 2, :], in_=h2[bt * P:(bt + 1) * P, :])
+        xT = {}
         wn = {}
 
         def load_w(g):
             wn[g] = wpool.tile([P, NB, 512], BF16, name="wn", tag="wn")
             nc.sync.dma_start(out=wn[g][:], in_=w1[:, g * 512:(g + 1) * 512].rearrange("(t p) k -> p t k", p=P))
 
-        for g in range(4):
+        for g in range(2):
             load_w(g)
 
         wc = const.tile([P, NG, F], U32, name="wc", align_bytes=64)
@@ -75,46 +78,37 @@ def tile_roibaseline_pa_kernel(tc, h_enc, enc_gamma, enc_beta, w1, b1, out):
         gamma = gbf[:, 0:40]
         beta = gbf[:, 64:104]
 
-        banks = {"n": 0}
-
-        def keep_clock(bank):
-            banks["n"] = banks["n"] + 1
-            if banks["n"] % 2 == 0 and banks["on"]:
-                nc.tensor.matmul(out=bank[:], lhsT=hn[0][:, 0:P], rhs=hn[0][:, 0:512], start=True, stop=True)
-
-        banks["on"] = True
-
-        def unit_bank(pool, tag, q, jj):
-            xs = pool.tile([P, 512], F32, name="xs", tag=tag)
-            keep_clock(xs)
+        def unit_bank(q, jj):
+            xs = psa.tile([P, 512], F32, name="xs", tag="xa")
             for i2 in range(2):
                 for bb in range(2):
                     j = 2 * jj + i2
                     nc.tensor.transpose(
                         out=xs[:, 256 * i2 + P * bb:256 * i2 + P * bb + P],
-                        in_=hn[2 * q + bb][:].bitcast(F32)[:, P * j:P * j + P],
+                        in_=hp[q][:, bb, :].bitcast(F32)[:, P * j:P * j + P],
                         identity=ident[:])
-            return xs[:].bitcast(BF16)
+            return xs
 
         def v_unit(q, jj):
-            xb = unit_bank(psb, "xb", q, jj)
+            xs = unit_bank(q, jj)
+            nc.scalar.copy(out=xT[q][:, jj, :].bitcast(F32), in_=xs[:])
             for i2 in range(2):
-                nc.vector.bn_stats(out=st[:, 2 * jj + i2, q, 0:6], in_=xb[:, 512 * i2:512 * i2 + 512])
+                nc.vector.bn_stats(out=st[:, 2 * jj + i2, q, 0:6], in_=xT[q][:, jj, 512 * i2:512 * i2 + 512])
 
         def s_unit(q, jj):
-            xv = unit_bank(psa, "xa", q, jj).rearrange("p (i c e) -> p i c e", i=2, e=2)
+            xv = unit_bank(q, jj)[:].bitcast(BF16).rearrange("p (i c e) -> p i c e", i=2, e=2)
+            xpl = xT[q][:, jj, :].rearrange("p (i e c) -> p i e c", i=2, e=2)
             s1 = spool.tile([P, 4], F32, name="s1", tag="s1")
             for i2 in range(2):
                 for e in range(2):
-                    junk = spool.tile([P, 256], BF16, name="junk", tag="junk")
-                    nc.scalar.activation(out=junk[:], in_=xv[:, i2, :, e], func=ACT.Identity,
+                    nc.scalar.activation(out=xpl[:, i2, e, :], in_=xv[:, i2, :, e], func=ACT.Identity,
                                          accum_out=s1[:, 2 * i2 + e:2 * i2 + e + 1])
             nc.scalar.activation(out=st[:, 2 * jj:2 * jj + 2, q, 1:5:3],
                                  in_=s1[:].rearrange("p (i e) -> p i e", e=2), func=ACT.Copy, scale=1.0 / 256.0)
             for i2 in range(2):
                 for e in range(2):
                     junk = spool.tile([P, 256], BF16, name="junk", tag="junk")
-                    nc.scalar.activation(out=junk[:], in_=xv[:, i2, :, e], func=ACT.Square, scale=-1.0,
+                    nc.scalar.activation(out=junk[:], in_=xpl[:, i2, e, :], func=ACT.Square, scale=-1.0,
                                          bias=st[:, 2 * jj + i2, q, 3 * e + 1:3 * e + 2],
                                          accum_out=st[:, 2 * jj + i2, q, 3 * e + 2:3 * e + 3])
 
@@ -126,7 +120,6 @@ def tile_roibaseline_pa_kernel(tc, h_enc, enc_gamma, enc_beta, w1, b1, out):
             w32 = wn[g][:].bitcast(F32)
             for wq in range(4):
                 wt = psa.tile([P, 512], F32, name="wt", tag="xa")
-                keep_clock(wt)
                 for u in range(2):
                     for f2 in range(2):
                         nc.tensor.transpose(
@@ -135,8 +128,8 @@ def tile_roibaseline_pa_kernel(tc, h_enc, enc_gamma, enc_beta, w1, b1, out):
                             identity=ident[:])
                 nc.scalar.copy(out=gw32[:, 256 * wq:256 * wq + 256, :],
                                in_=wt[:].rearrange("p (u f) -> p f u", u=2))
-            if g + 4 < NG:
-                load_w(g + 4)
+            if g + 2 < NG:
+                load_w(g + 2)
 
         def w_quant(g):
             nc.vector.quantize_mx(out=wc[:, g, :].bitcast(FP8X4), scales=ws[:, g, :], in_=gws[g][:])
@@ -154,51 +147,42 @@ def tile_roibaseline_pa_kernel(tc, h_enc, enc_gamma, enc_beta, w1, b1, out):
 
         nv = 0
         for q in range(4):
+            xT[q] = big.tile([P, 10, 1024], BF16, name="xT", tag="hx")
             for i in range(8):
-                if i == (2 if q == 0 else 0):
+                if i == 2:
                     s_unit(q, 8)
+                if i == 6:
                     s_unit(q, 9)
                 v_unit(q, i)
                 nv += 1
-                if nv >= 20 and nv % 2 == 0:
+                if nv >= 28 and nv % 2 == 0:
                     w_slot_group()
                     w_slot_quant()
 
-        xts = {}
         nts = {}
         gcs = {}
         ccs = {}
         accs = {}
 
-        def t_step(d):
+        def a_step(d):
             r, gp = d // 5, d % 5
             for gg in range(2):
                 g = 2 * gp + gg
-                xt = psa.tile([P, 512], F32, name="xt", tag="xa")
-                xts[(d, gg)] = xt
-                for u in range(2):
-                    for bb in range(2):
-                        nc.tensor.transpose(
-                            out=xt[:, 256 * u + P * bb:256 * u + P * bb + P],
-                            in_=hn[2 * r + bb][:].bitcast(F32)[:, P * (2 * g + u):P * (2 * g + u) + P],
-                            identity=ident[:])
-
-        def a_step(d):
-            gp = d % 5
-            for gg in range(2):
-                g = 2 * gp + gg
-                xv = xts[(d, gg)][:].bitcast(BF16).rearrange("p (u c e) -> p u c e", u=2, e=2)
+                if g < 8:
+                    xv = xT[r][:, g, :].rearrange("p (u c e) -> p u e c", u=2, e=2)
+                else:
+                    xv = xT[r][:, g, :].rearrange("p (u e c) -> p u e c", u=2, e=2)
                 nt = npool.tile([P, 4, 256], F32, name="nt", tag="nt")
                 nts[(d, gg)] = nt
                 for u in range(2):
                     for e in range(2):
                         je = 2 * (2 * g + u) + e
-                        nc.scalar.activation(out=nt[:, 2 * u + e, :], in_=xv[:, u, :, e], func=ACT.Identity,
+                        nc.scalar.activation(out=nt[:, 2 * u + e, :], in_=xv[:, u, e, :], func=ACT.Identity,
                                              scale=sa[:, je:je + 1], bias=sb[:, je:je + 1])
 
         def l_step(d, gg):
             if gg == 0:
-                gcs[d] = cpool.tile([P, 2048], BF16, name="gc", tag="gc", align_bytes=64)
+                gcs[d] = gcpool.tile([P, 2048], BF16, name="gc", tag="gc", align_bytes=64)
             nv4 = nts[(d, gg)][:].rearrange("p t c -> p c t")
             nc.vector.scalar_tensor_tensor(
                 out=gcs[d][:, 1024 * gg:1024 * gg + 1024].rearrange("p (c t) -> p c t", t=4),
@@ -269,7 +253,6 @@ def tile_roibaseline_pa_kernel(tc, h_enc, enc_gamma, enc_beta, w1, b1, out):
         nc.scalar.activation(out=sd[:], in_=veps[:], func=ACT.Sqrt)
         w_slot_group()
         w_slot_quant()
-        t_step(0)
         nc.vector.reciprocal(out=r0[:], in_=sd[:])
         nc.vector.tensor_tensor(out=vr[:], in0=veps[:], in1=r0[:], op=ALU.mult)
         nc.vector.tensor_tensor(out=s2[:], in0=vr[:], in1=sd[:], op=ALU.add)
@@ -279,13 +262,10 @@ def tile_roibaseline_pa_kernel(tc, h_enc, enc_gamma, enc_beta, w1, b1, out):
         nc.vector.tensor_tensor(out=sb[:], in0=beta, in1=ma[:], op=ALU.subtract)
         nc.sync.dma_start(out=bias[:], in_=b1.partition_broadcast(P))
 
-        banks["on"] = False
         for p in range(ND + 3):
             if p < ND:
                 a_step(p)
             w_slot_group()
-            if p + 1 < ND:
-                t_step(p + 1)
             if 1 <= p <= ND:
                 l_step(p - 1, 0)
             if p >= 7 and (p - 7) % 5 == 0:

@@ -8,272 +8,274 @@ U8 = mybir.dt.uint8
 FP8X4 = mybir.dt.float8_e4m3fn_x4
 ALU = mybir.AluOpType
 ACT = mybir.ActivationFunctionType
+AXIS_X = mybir.AxisListType.X
 
 P = 128
 B = 1024
 C = 5120
 F = 1024
-NB = B // P
-NJ = C // 256
-NG = C // 512
 EPS = 1e-5
 SLOPE = 0.3
 FLOPS = 2 * B * C * F
-ND = 20
+
+K_PASS = 512
+PASSES = C // K_PASS
+PAIRS = B // (2 * P)
+ROWS = 2 * P
+BANK = 512
+V_PASSES = 8
+STEPS = PAIRS * PASSES // 2
+W_AHEAD = 4
+W_FIRST_UNIT = 28
 
 
 def tile_roibaseline_pa_kernel(tc, h_enc, enc_gamma, enc_beta, w1, b1, out):
     nc = tc.nc
     h2 = h_enc.rearrange("b r o -> b (r o)")
-    with tc.tile_pool(name="const", bufs=1) as const, \
-            tc.tile_pool(name="big", bufs=5) as big, \
-            tc.tile_pool(name="wpool", bufs=2) as wpool, \
-            tc.tile_pool(name="gpool", bufs=2) as gpool, \
-            tc.tile_pool(name="spool", bufs=2) as spool, \
-            tc.tile_pool(name="npool", bufs=4) as npool, \
-            tc.tile_pool(name="gcpool", bufs=2) as gcpool, \
-            tc.tile_pool(name="cpool", bufs=3) as cpool, \
-            tc.tile_pool(name="opool", bufs=3) as opool, \
-            tc.psum_pool(name="psa", bufs=4) as psa, \
-            tc.psum_pool(name="psb", bufs=4) as psb, \
+    with tc.tile_pool(name="keep", bufs=1) as keep, \
+            tc.tile_pool(name="w_in", bufs=4) as w_in, \
+            tc.tile_pool(name="w_grouped", bufs=2) as w_grouped, \
+            tc.tile_pool(name="scalar_stats", bufs=2) as scalar_stats, \
+            tc.tile_pool(name="normed", bufs=4) as normed, \
+            tc.tile_pool(name="c_tiles", bufs=3) as c_tiles, \
+            tc.tile_pool(name="result", bufs=3) as result, \
+            tc.psum_pool(name="psum_a", bufs=4) as psum_a, \
+            tc.psum_pool(name="psum_b", bufs=4) as psum_b, \
             tc.manual_schedule():
-        ident = const.tile([P, P], F32, name="ident")
+        ident = keep.tile([P, P], F32, name="ident")
         make_identity(nc, ident[:])
-        one = const.tile([P, 1], F32, name="one")
+        one = keep.tile([P, 1], F32, name="one")
         nc.vector.memset(one[:], 1.0)
-        warm = const.tile([P, 1], F32, name="warm")
-        nc.scalar.activation(out=warm[:], in_=one[:], func=ACT.Sqrt)
-        gbn = const.tile([P, 256], BF16, name="gbn")
-        nc.vector.memset(gbn[:], 0.0)
-        st = const.tile([P, NJ, 4, 8], F32, name="st")
-        nc.vector.memset(st[:], 256.0)
+        sqrt_one = keep.tile([P, 1], F32, name="sqrt_one")
+        nc.scalar.activation(out=sqrt_one[:], in_=one[:], func=ACT.Sqrt)
 
-        nc.sync.dma_start(out=gbn[0:20, :], in_=enc_gamma.rearrange("(j x) o -> j (x o)", j=NJ))
-        nc.sync.dma_start(out=gbn[32:52, :], in_=enc_beta.rearrange("(j x) o -> j (x o)", j=NJ))
-        hp = [big.tile([P, 2, C], BF16, name="hp", tag="hx") for q in range(4)]
-        for ch in (0, 4, 1, 2, 3):
+        gb_rows = keep.tile([P, 2 * P], BF16, name="gb_rows")
+        nc.vector.memset(gb_rows[:], 0.0)
+        nc.sync.dma_start(out=gb_rows[0:20, :], in_=enc_gamma.rearrange("(j x) o -> j (x o)", j=2 * PASSES))
+        nc.sync.dma_start(out=gb_rows[32:52, :], in_=enc_beta.rearrange("(j x) o -> j (x o)", j=2 * PASSES))
+        h_sb = [keep.tile([P, C], BF16, name="h_sb%d" % bt) for bt in range(2 * PAIRS)]
+        for piece in (0, 4, 1, 2, 3):
+            cols = slice(2 * K_PASS * piece, 2 * K_PASS * (piece + 1))
             for bt in range(2):
-                nc.sync.dma_start(out=hp[0][:, bt, 1024 * ch:1024 * ch + 1024],
-                                  in_=h2[bt * P:(bt + 1) * P, 1024 * ch:1024 * ch + 1024])
-        for bt in range(2, NB):
-            nc.sync.dma_start(out=hp[bt // 2][:, bt % 2, :], in_=h2[bt * P:(bt + 1) * P, :])
-        xT = {}
-        wn = {}
+                nc.sync.dma_start(out=h_sb[bt][:, cols], in_=h2[bt * P:(bt + 1) * P, cols])
+        for bt in range(2, 2 * PAIRS):
+            nc.sync.dma_start(out=h_sb[bt][:], in_=h2[bt * P:(bt + 1) * P, :])
+        w_sb = {}
 
         def load_w(g):
-            wn[g] = wpool.tile([P, NB, 512], BF16, name="wn", tag="wn")
-            nc.sync.dma_start(out=wn[g][:], in_=w1[:, g * 512:(g + 1) * 512].rearrange("(t p) k -> p t k", p=P))
+            w_sb[g] = w_in.tile([P, F // P, K_PASS], BF16, name="w_sb", tag="w_sb")
+            nc.sync.dma_start(out=w_sb[g][:],
+                              in_=w1[:, g * K_PASS:(g + 1) * K_PASS].rearrange("(f p) k -> p f k", p=P))
 
-        for g in range(2):
+        for g in range(4):
             load_w(g)
 
-        wc = const.tile([P, NG, F], U32, name="wc", align_bytes=64)
-        ws = const.tile([P, NG, F], U8, name="ws", align_bytes=64)
-        bias = const.tile([P, F], BF16, name="bias")
+        w_codes = keep.tile([P, PASSES, F], U32, name="w_codes", align_bytes=64)
+        w_scales = keep.tile([P, PASSES, F], U8, name="w_scales", align_bytes=64)
+        bias = keep.tile([P, F], BF16, name="bias")
 
-        gps = psa.tile([P, 512], F32, name="gps", tag="xa")
-        nc.tensor.transpose(out=gps[:, 0:P], in_=gbn[:].bitcast(F32), identity=ident[:])
-        gbf = const.tile([P, P], F32, name="gbf")
-        nc.vector.tensor_copy(out=gbf[:], in_=gps[:].bitcast(BF16)[:, 0:P])
-        gamma = gbf[:, 0:40]
-        beta = gbf[:, 64:104]
+        gb_bank = psum_a.tile([P, BANK], F32, name="gb_bank", tag="a")
+        nc.tensor.transpose(out=gb_bank[:, 0:P], in_=gb_rows[:].bitcast(F32), identity=ident[:])
+        gb = keep.tile([P, P], F32, name="gb")
+        nc.vector.tensor_copy(out=gb[:], in_=gb_bank[:].bitcast(BF16)[:, 0:P])
+        gamma = gb[:, 0:4 * PASSES]
+        beta = gb[:, 64:64 + 4 * PASSES]
 
-        def unit_bank(q, jj):
-            xs = psa.tile([P, 512], F32, name="xs", tag="xa")
-            for i2 in range(2):
+        def transpose_h(bank, q, g):
+            for u in range(2):
                 for bb in range(2):
-                    j = 2 * jj + i2
-                    nc.tensor.transpose(
-                        out=xs[:, 256 * i2 + P * bb:256 * i2 + P * bb + P],
-                        in_=hp[q][:, bb, :].bitcast(F32)[:, P * j:P * j + P],
-                        identity=ident[:])
-            return xs
+                    word0 = P * (2 * g + u)
+                    nc.tensor.transpose(out=bank[:, ROWS * u + P * bb:ROWS * u + P * bb + P],
+                                        in_=h_sb[2 * q + bb][:].bitcast(F32)[:, word0:word0 + P],
+                                        identity=ident[:])
 
-        def v_unit(q, jj):
-            xs = unit_bank(q, jj)
-            nc.scalar.copy(out=xT[q][:, jj, :].bitcast(F32), in_=xs[:])
-            for i2 in range(2):
-                nc.vector.bn_stats(out=st[:, 2 * jj + i2, q, 0:6], in_=xT[q][:, jj, 512 * i2:512 * i2 + 512])
+        stats = keep.tile([P, PASSES, 2, PAIRS, 8], F32, name="stats")
 
-        def s_unit(q, jj):
-            xv = unit_bank(q, jj)[:].bitcast(BF16).rearrange("p (i c e) -> p i c e", i=2, e=2)
-            xpl = xT[q][:, jj, :].rearrange("p (i e c) -> p i e c", i=2, e=2)
-            s1 = spool.tile([P, 4], F32, name="s1", tag="s1")
-            for i2 in range(2):
+        def vector_unit(q, g):
+            bank = psum_b.tile([P, BANK], F32, name="v_bank", tag="b")
+            transpose_h(bank, q, g)
+            for u in range(2):
+                nc.vector.bn_stats(out=stats[:, g, u, q, 0:6],
+                                   in_=bank[:].bitcast(BF16)[:, 2 * ROWS * u:2 * ROWS * (u + 1)])
+
+        def scalar_unit(q, g):
+            bank = psum_a.tile([P, BANK], F32, name="s_bank", tag="a")
+            transpose_h(bank, q, g)
+            x = bank[:].bitcast(BF16).rearrange("p (u r e) -> p u r e", u=2, e=2)
+            sums = scalar_stats.tile([P, 4], F32, name="sums", tag="sums")
+            for u in range(2):
                 for e in range(2):
-                    nc.scalar.activation(out=xpl[:, i2, e, :], in_=xv[:, i2, :, e], func=ACT.Identity,
-                                         accum_out=s1[:, 2 * i2 + e:2 * i2 + e + 1])
-            nc.scalar.activation(out=st[:, 2 * jj:2 * jj + 2, q, 1:5:3],
-                                 in_=s1[:].rearrange("p (i e) -> p i e", e=2), func=ACT.Copy, scale=1.0 / 256.0)
-            for i2 in range(2):
+                    unused = scalar_stats.tile([P, ROWS], BF16, name="unused", tag="unused")
+                    nc.scalar.activation(out=unused[:], in_=x[:, u, :, e], func=ACT.Identity,
+                                         accum_out=sums[:, 2 * u + e:2 * u + e + 1])
+            nc.scalar.activation(out=stats[:, g, :, q, 1:5:3], in_=sums[:].rearrange("p (u e) -> p u e", e=2),
+                                 func=ACT.Copy, scale=1.0 / ROWS)
+            for u in range(2):
                 for e in range(2):
-                    junk = spool.tile([P, 256], BF16, name="junk", tag="junk")
-                    nc.scalar.activation(out=junk[:], in_=xpl[:, i2, e, :], func=ACT.Square, scale=-1.0,
-                                         bias=st[:, 2 * jj + i2, q, 3 * e + 1:3 * e + 2],
-                                         accum_out=st[:, 2 * jj + i2, q, 3 * e + 2:3 * e + 3])
+                    unused = scalar_stats.tile([P, ROWS], BF16, name="unused", tag="unused")
+                    nc.scalar.activation(out=unused[:], in_=x[:, u, :, e], func=ACT.Square, scale=-1.0,
+                                         bias=stats[:, g, u, q, 3 * e + 1:3 * e + 2],
+                                         accum_out=stats[:, g, u, q, 3 * e + 2:3 * e + 3])
 
-        gws = {}
+        w_bf = {}
 
         def w_group(g):
-            gws[g] = gpool.tile([P, 4 * F], BF16, name="gw", tag="gw", align_bytes=64)
-            gw32 = gws[g][:].bitcast(F32).rearrange("p (f u) -> p f u", u=2)
-            w32 = wn[g][:].bitcast(F32)
-            for wq in range(4):
-                wt = psa.tile([P, 512], F32, name="wt", tag="xa")
+            w_bf[g] = w_grouped.tile([P, 4 * F], BF16, name="w_bf", tag="w_bf", align_bytes=64)
+            grouped = w_bf[g][:].bitcast(F32).rearrange("p (f u) -> p f u", u=2)
+            words = w_sb[g][:].bitcast(F32)
+            for part in range(4):
+                bank = psum_a.tile([P, BANK], F32, name="w_bank", tag="a")
                 for u in range(2):
-                    for f2 in range(2):
-                        nc.tensor.transpose(
-                            out=wt[:, 256 * u + P * f2:256 * u + P * f2 + P],
-                            in_=w32[:, 2 * wq + f2, P * u:P * u + P],
-                            identity=ident[:])
-                nc.scalar.copy(out=gw32[:, 256 * wq:256 * wq + 256, :],
-                               in_=wt[:].rearrange("p (u f) -> p f u", u=2))
-            if g + 2 < NG:
-                load_w(g + 2)
+                    for ft in range(2):
+                        nc.tensor.transpose(out=bank[:, 2 * P * u + P * ft:2 * P * u + P * ft + P],
+                                            in_=words[:, 2 * part + ft, P * u:P * u + P], identity=ident[:])
+                nc.scalar.copy(out=grouped[:, 2 * P * part:2 * P * (part + 1), :],
+                               in_=bank[:].rearrange("p (u f) -> p f u", u=2))
+            if g + 4 < PASSES:
+                load_w(g + 4)
 
-        def w_quant(g):
-            nc.vector.quantize_mx(out=wc[:, g, :].bitcast(FP8X4), scales=ws[:, g, :], in_=gws[g][:])
+        def w_quantise(g):
+            nc.vector.quantize_mx(out=w_codes[:, g, :].bitcast(FP8X4), scales=w_scales[:, g, :], in_=w_bf[g][:])
 
-        wstate = {"g": 0}
+        units = 0
+        for q in range(PAIRS):
+            for g in range(V_PASSES):
+                if g == 2:
+                    scalar_unit(q, V_PASSES)
+                if g == 6:
+                    scalar_unit(q, V_PASSES + 1)
+                vector_unit(q, g)
+                units += 1
+                if units >= W_FIRST_UNIT and units % 2 == 0:
+                    w_group((units - W_FIRST_UNIT) // 2)
+                    if units > W_FIRST_UNIT:
+                        w_quantise((units - W_FIRST_UNIT) // 2 - 1)
 
-        def w_slot_group():
-            if wstate["g"] < NG:
-                w_group(wstate["g"])
+        chunk_mean = stats[:, :, :, :, 1:5:3].rearrange("p g u q e -> p (g u) e q")
+        chunk_m2 = stats[:, :, :, :, 2:6:3].rearrange("p g u q e -> p (g u) e q")
+        shape3 = [P, 2 * PASSES, 2]
+        mean_sum = keep.tile(shape3, F32, name="mean_sum")
+        mean = keep.tile(shape3, F32, name="mean")
+        m2_sum = keep.tile(shape3, F32, name="m2_sum")
+        dist = keep.tile(shape3 + [PAIRS], F32, name="dist")
+        dist2 = keep.tile(shape3 + [PAIRS], F32, name="dist2")
+        dist2_sum = keep.tile(shape3, F32, name="dist2_sum")
+        flat = [P, 4 * PASSES]
+        within = keep.tile(flat, F32, name="within")
+        var_eps = keep.tile(flat, F32, name="var_eps")
+        root = keep.tile(flat, F32, name="root")
+        inv_root = keep.tile(flat, F32, name="inv_root")
+        quotient = keep.tile(flat, F32, name="quotient")
+        two_roots = keep.tile(flat, F32, name="two_roots")
+        inv_two_roots = keep.tile(flat, F32, name="inv_two_roots")
+        scale = keep.tile(flat, F32, name="scale")
+        mean_scaled = keep.tile(flat, F32, name="mean_scaled")
+        offset = keep.tile(flat, F32, name="offset")
+        nc.vector.tensor_reduce(out=mean_sum[:], in_=chunk_mean, axis=AXIS_X, op=ALU.add)
+        nc.vector.tensor_reduce(out=m2_sum[:], in_=chunk_m2, axis=AXIS_X, op=ALU.add)
+        nc.vector.tensor_scalar_mul(out=mean[:], in0=mean_sum[:], scalar1=1.0 / PAIRS)
+        nc.vector.tensor_scalar(out=within[:], in0=m2_sum[:].rearrange("p j e -> p (j e)"), scalar1=1.0 / B,
+                                scalar2=EPS, op0=ALU.mult, op1=ALU.add)
+        nc.vector.tensor_tensor(out=dist[:], in0=chunk_mean,
+                                in1=mean[:].unsqueeze(3).to_broadcast(shape3 + [PAIRS]), op=ALU.subtract)
+        nc.vector.tensor_tensor(out=dist2[:], in0=dist[:], in1=dist[:], op=ALU.mult)
+        nc.vector.tensor_reduce(out=dist2_sum[:], in_=dist2[:], axis=AXIS_X, op=ALU.add)
+        nc.vector.scalar_tensor_tensor(out=var_eps[:], in0=dist2_sum[:].rearrange("p j e -> p (j e)"),
+                                       scalar=1.0 / PAIRS, in1=within[:], op0=ALU.mult, op1=ALU.add)
+        nc.scalar.activation(out=root[:], in_=var_eps[:], func=ACT.Sqrt)
+        w_group(W_AHEAD - 1)
+        w_quantise(W_AHEAD - 2)
 
-        def w_slot_quant():
-            if 1 <= wstate["g"] <= NG:
-                w_quant(wstate["g"] - 1)
-            wstate["g"] = wstate["g"] + 1
+        x_banks = {}
+        n_tiles = {}
+        c_bf = {}
+        c_mx = {}
+        acc = {}
 
-        nv = 0
-        for q in range(4):
-            xT[q] = big.tile([P, 10, 1024], BF16, name="xT", tag="hx")
-            for i in range(8):
-                if i == 2:
-                    s_unit(q, 8)
-                if i == 6:
-                    s_unit(q, 9)
-                v_unit(q, i)
-                nv += 1
-                if nv >= 28 and nv % 2 == 0:
-                    w_slot_group()
-                    w_slot_quant()
+        def transposes(d):
+            for half in range(2):
+                x_banks[(d, half)] = psum_a.tile([P, BANK], F32, name="x_bank", tag="a")
+                transpose_h(x_banks[(d, half)], d // 5, 2 * (d % 5) + half)
 
-        nts = {}
-        gcs = {}
-        ccs = {}
-        accs = {}
-
-        def a_step(d):
-            r, gp = d // 5, d % 5
-            for gg in range(2):
-                g = 2 * gp + gg
-                if g < 8:
-                    xv = xT[r][:, g, :].rearrange("p (u c e) -> p u e c", u=2, e=2)
-                else:
-                    xv = xT[r][:, g, :].rearrange("p (u e c) -> p u e c", u=2, e=2)
-                nt = npool.tile([P, 4, 256], F32, name="nt", tag="nt")
-                nts[(d, gg)] = nt
+        def norm(d):
+            for half in range(2):
+                g = 2 * (d % 5) + half
+                x = x_banks[(d, half)][:].bitcast(BF16).rearrange("p (u r e) -> p u r e", u=2, e=2)
+                n_tiles[(d, half)] = normed.tile([P, 4, ROWS], F32, name="n_tile", tag="n_tile")
                 for u in range(2):
                     for e in range(2):
-                        je = 2 * (2 * g + u) + e
-                        nc.scalar.activation(out=nt[:, 2 * u + e, :], in_=xv[:, u, e, :], func=ACT.Identity,
-                                             scale=sa[:, je:je + 1], bias=sb[:, je:je + 1])
+                        col = 4 * g + 2 * u + e
+                        nc.scalar.activation(out=n_tiles[(d, half)][:, 2 * u + e, :], in_=x[:, u, :, e],
+                                             func=ACT.Identity, scale=scale[:, col:col + 1],
+                                             bias=offset[:, col:col + 1])
 
-        def l_step(d, gg):
-            if gg == 0:
-                gcs[d] = gcpool.tile([P, 2048], BF16, name="gc", tag="gc", align_bytes=64)
-            nv4 = nts[(d, gg)][:].rearrange("p t c -> p c t")
+        def leaky_relu(d, half):
+            if half == 0:
+                c_bf[d] = c_tiles.tile([P, 8 * ROWS], BF16, name="c_bf", tag="c_bf", align_bytes=64)
+            n = n_tiles[(d, half)][:].rearrange("p t r -> p r t")
             nc.vector.scalar_tensor_tensor(
-                out=gcs[d][:, 1024 * gg:1024 * gg + 1024].rearrange("p (c t) -> p c t", t=4),
-                in0=nv4, scalar=SLOPE, in1=nv4, op0=ALU.mult, op1=ALU.max)
+                out=c_bf[d][:, 4 * ROWS * half:4 * ROWS * (half + 1)].rearrange("p (r t) -> p r t", t=4),
+                in0=n, scalar=SLOPE, in1=n, op0=ALU.mult, op1=ALU.max)
 
-        def q_step(d):
-            cc = cpool.tile([P, 512], U32, name="cc", tag="cc", align_bytes=64)
-            cs = cpool.tile([P, 512], U8, name="cs", tag="cs", align_bytes=64)
-            ccs[d] = (cc, cs)
-            nc.vector.quantize_mx(out=cc[:].bitcast(FP8X4), scales=cs[:], in_=gcs[d][:])
+        def quantise(d):
+            codes = c_tiles.tile([P, 2 * ROWS], U32, name="c_codes", tag="c_codes", align_bytes=64)
+            scales = c_tiles.tile([P, 2 * ROWS], U8, name="c_scales", tag="c_scales", align_bytes=64)
+            c_mx[d] = (codes, scales)
+            nc.vector.quantize_mx(out=codes[:].bitcast(FP8X4), scales=scales[:], in_=c_bf[d][:])
 
-        def m_step(d):
-            r, gp = d // 5, d % 5
-            if gp == 0:
-                accs[r] = [[psb.tile([P, 512], F32, name="acc", tag="xb") for fh in range(2)] for bb in range(2)]
-            cc, cs = ccs[d]
+        def mx_passes(d):
+            r = d // 5
+            if d % 5 == 0:
+                acc[r] = [[psum_b.tile([P, BANK], F32, name="acc", tag="b") for fh in range(2)] for bb in range(2)]
+            codes, scales = c_mx[d]
             for bb in range(2):
                 for fh in range(2):
-                    for gg in range(2):
-                        g = 2 * gp + gg
-                        col = 256 * gg + P * bb
-                        nc.tensor.matmul_mx(
-                            out=accs[r][bb][fh][:],
-                            lhsT=cc[:, col:col + P].bitcast(FP8X4), lhsT_scale=cs[:, col:col + P],
-                            rhs=wc[:, g, 512 * fh:512 * fh + 512].bitcast(FP8X4),
-                            rhs_scale=ws[:, g, 512 * fh:512 * fh + 512],
-                            start=(g == 0), stop=(g == NG - 1))
+                    for half in range(2):
+                        g = 2 * (d % 5) + half
+                        rows = slice(ROWS * half + P * bb, ROWS * half + P * bb + P)
+                        outs = slice(BANK * fh, BANK * (fh + 1))
+                        nc.tensor.matmul_mx(out=acc[r][bb][fh][:],
+                                            lhsT=codes[:, rows].bitcast(FP8X4), lhsT_scale=scales[:, rows],
+                                            rhs=w_codes[:, g, outs].bitcast(FP8X4), rhs_scale=w_scales[:, g, outs],
+                                            start=(g == 0), stop=(g == PASSES - 1))
 
-        def e_step(r):
+        def add_bias_and_store(r):
             for bb in range(2):
                 for fh in range(2):
-                    ob = opool.tile([P, 512], F32, name="ob", tag="ob")
-                    nc.vector.tensor_tensor(out=ob[:], in0=accs[r][bb][fh][:],
-                                            in1=bias[:, 512 * fh:512 * fh + 512], op=ALU.add)
-                    row = (2 * r + bb) * P
-                    nc.sync.dma_start(out=out[row:row + P, 512 * fh:512 * fh + 512], in_=ob[:])
+                    outs = slice(BANK * fh, BANK * (fh + 1))
+                    res = result.tile([P, BANK], F32, name="res", tag="res")
+                    nc.vector.tensor_tensor(out=res[:], in0=acc[r][bb][fh][:], in1=bias[:, outs], op=ALU.add)
+                    row0 = (2 * r + bb) * P
+                    nc.sync.dma_start(out=out[row0:row0 + P, outs], in_=res[:])
 
-        mq = st[:, :, :, 1:5:3].rearrange("p j q e -> p j e q")
-        m2q = st[:, :, :, 2:6:3].rearrange("p j q e -> p j e q")
-        msum = const.tile([P, NJ, 2], F32, name="msum")
-        mean3 = const.tile([P, NJ, 2], F32, name="mean3")
-        dq = const.tile([P, NJ, 2, 4], F32, name="dq")
-        dd = const.tile([P, NJ, 2, 4], F32, name="dd")
-        r1 = const.tile([P, NJ, 2], F32, name="r1")
-        r2 = const.tile([P, NJ, 2], F32, name="r2")
-        v1 = const.tile([P, 40], F32, name="v1")
-        nc.vector.tensor_reduce(out=msum[:], in_=mq, axis=mybir.AxisListType.X, op=ALU.add)
-        nc.vector.tensor_reduce(out=r1[:], in_=m2q, axis=mybir.AxisListType.X, op=ALU.add)
-        nc.vector.tensor_scalar_mul(out=mean3[:], in0=msum[:], scalar1=0.25)
-        nc.vector.tensor_scalar(out=v1[:], in0=r1[:].rearrange("p j e -> p (j e)"), scalar1=1.0 / B, scalar2=EPS,
-                                op0=ALU.mult, op1=ALU.add)
-        nc.vector.tensor_tensor(out=dq[:], in0=mq, in1=mean3[:].unsqueeze(3).to_broadcast([P, NJ, 2, 4]),
-                                op=ALU.subtract)
-        nc.vector.tensor_tensor(out=dd[:], in0=dq[:], in1=dq[:], op=ALU.mult)
-        nc.vector.tensor_reduce(out=r2[:], in_=dd[:], axis=mybir.AxisListType.X, op=ALU.add)
-        mean = mean3[:].rearrange("p j e -> p (j e)")
-        veps = const.tile([P, 40], F32, name="veps")
-        sd = const.tile([P, 40], F32, name="sd")
-        r0 = const.tile([P, 40], F32, name="r0")
-        vr = const.tile([P, 40], F32, name="vr")
-        s2 = const.tile([P, 40], F32, name="s2")
-        rs = const.tile([P, 40], F32, name="rs")
-        sa = const.tile([P, 40], F32, name="sa")
-        ma = const.tile([P, 40], F32, name="ma")
-        sb = const.tile([P, 40], F32, name="sb")
-        nc.vector.scalar_tensor_tensor(out=veps[:], in0=r2[:].rearrange("p j e -> p (j e)"), scalar=0.25, in1=v1[:],
-                                       op0=ALU.mult, op1=ALU.add)
-        nc.scalar.activation(out=sd[:], in_=veps[:], func=ACT.Sqrt)
-        w_slot_group()
-        w_slot_quant()
-        nc.vector.reciprocal(out=r0[:], in_=sd[:])
-        nc.vector.tensor_tensor(out=vr[:], in0=veps[:], in1=r0[:], op=ALU.mult)
-        nc.vector.tensor_tensor(out=s2[:], in0=vr[:], in1=sd[:], op=ALU.add)
-        nc.vector.reciprocal(out=rs[:], in_=s2[:])
-        nc.vector.scalar_tensor_tensor(out=sa[:], in0=gamma, scalar=2.0, in1=rs[:], op0=ALU.mult, op1=ALU.mult)
-        nc.vector.tensor_tensor(out=ma[:], in0=mean, in1=sa[:], op=ALU.mult)
-        nc.vector.tensor_tensor(out=sb[:], in0=beta, in1=ma[:], op=ALU.subtract)
+        transposes(0)
+        nc.vector.reciprocal(out=inv_root[:], in_=root[:])
+        nc.vector.tensor_tensor(out=quotient[:], in0=var_eps[:], in1=inv_root[:], op=ALU.mult)
+        nc.vector.tensor_tensor(out=two_roots[:], in0=quotient[:], in1=root[:], op=ALU.add)
+        nc.vector.reciprocal(out=inv_two_roots[:], in_=two_roots[:])
+        nc.vector.scalar_tensor_tensor(out=scale[:], in0=gamma, scalar=2.0, in1=inv_two_roots[:],
+                                       op0=ALU.mult, op1=ALU.mult)
+        nc.vector.tensor_tensor(out=mean_scaled[:], in0=mean[:].rearrange("p j e -> p (j e)"), in1=scale[:],
+                                op=ALU.mult)
+        nc.vector.tensor_tensor(out=offset[:], in0=beta, in1=mean_scaled[:], op=ALU.subtract)
         nc.sync.dma_start(out=bias[:], in_=b1.partition_broadcast(P))
 
-        for p in range(ND + 3):
-            if p < ND:
-                a_step(p)
-            w_slot_group()
-            if 1 <= p <= ND:
-                l_step(p - 1, 0)
+        for p in range(STEPS + 3):
+            if p < STEPS:
+                norm(p)
+            if p + W_AHEAD < PASSES:
+                w_group(p + W_AHEAD)
+            if p + 1 < STEPS:
+                transposes(p + 1)
+            if 1 <= p <= STEPS:
+                leaky_relu(p - 1, 0)
             if p >= 7 and (p - 7) % 5 == 0:
-                e_step((p - 7) // 5)
-            if 2 <= p <= ND + 1:
-                q_step(p - 2)
-            if 1 <= p <= ND:
-                l_step(p - 1, 1)
-            w_slot_quant()
-            if 2 <= p <= ND + 1:
-                m_step(p - 2)
+                add_bias_and_store((p - 7) // 5)
+            if 2 <= p <= STEPS + 1:
+                quantise(p - 2)
+            if 1 <= p <= STEPS:
+                leaky_relu(p - 1, 1)
+            if p + W_AHEAD - 1 < PASSES:
+                w_quantise(p + W_AHEAD - 1)
+            if 2 <= p <= STEPS + 1:
+                mx_passes(p - 2)

import concourse.mybir as mybir
from concourse.masks import make_identity

F32 = mybir.dt.float32
BF16 = mybir.dt.bfloat16
U32 = mybir.dt.uint32
U8 = mybir.dt.uint8
FP8X4 = mybir.dt.float8_e4m3fn_x4
ALU = mybir.AluOpType
ACT = mybir.ActivationFunctionType
AXIS_X = mybir.AxisListType.X

P = 128
B = 1024
C = 5120
F = 1024
EPS = 1e-5
SLOPE = 0.3
FLOPS = 2 * B * C * F

K_PASS = 512
PASSES = C // K_PASS
PAIRS = B // (2 * P)
ROWS = 2 * P
BANK = 512
V_PASSES = 8
STEPS = PAIRS * PASSES // 2
W_AHEAD = 4
W_FIRST_UNIT = 28


def tile_roibaseline_pa_kernel(tc, h_enc, enc_gamma, enc_beta, w1, b1, out):
    nc = tc.nc
    h2 = h_enc.rearrange("b r o -> b (r o)")
    with tc.tile_pool(name="keep", bufs=1) as keep, \
            tc.tile_pool(name="w_in", bufs=4) as w_in, \
            tc.tile_pool(name="w_grouped", bufs=2) as w_grouped, \
            tc.tile_pool(name="scalar_stats", bufs=2) as scalar_stats, \
            tc.tile_pool(name="normed", bufs=4) as normed, \
            tc.tile_pool(name="c_tiles", bufs=3) as c_tiles, \
            tc.tile_pool(name="result", bufs=3) as result, \
            tc.psum_pool(name="psum_a", bufs=4) as psum_a, \
            tc.psum_pool(name="psum_b", bufs=4) as psum_b, \
            tc.manual_schedule():
        ident = keep.tile([P, P], F32, name="ident")
        make_identity(nc, ident[:])
        one = keep.tile([P, 1], F32, name="one")
        nc.vector.memset(one[:], 1.0)
        sqrt_one = keep.tile([P, 1], F32, name="sqrt_one")
        nc.scalar.activation(out=sqrt_one[:], in_=one[:], func=ACT.Sqrt)

        gb_rows = keep.tile([P, 2 * P], BF16, name="gb_rows")
        nc.vector.memset(gb_rows[:], 0.0)
        nc.sync.dma_start(out=gb_rows[0:20, :], in_=enc_gamma.rearrange("(j x) o -> j (x o)", j=2 * PASSES))
        nc.sync.dma_start(out=gb_rows[32:52, :], in_=enc_beta.rearrange("(j x) o -> j (x o)", j=2 * PASSES))
        h_sb = [keep.tile([P, C], BF16, name="h_sb%d" % bt) for bt in range(2 * PAIRS)]
        for piece in (0, 4, 1, 2, 3):
            cols = slice(2 * K_PASS * piece, 2 * K_PASS * (piece + 1))
            for bt in range(2):
                nc.sync.dma_start(out=h_sb[bt][:, cols], in_=h2[bt * P:(bt + 1) * P, cols])
        for bt in range(2, 2 * PAIRS):
            nc.sync.dma_start(out=h_sb[bt][:], in_=h2[bt * P:(bt + 1) * P, :])
        w_sb = {}

        def load_w(g):
            w_sb[g] = w_in.tile([P, F // P, K_PASS], BF16, name="w_sb", tag="w_sb")
            nc.sync.dma_start(out=w_sb[g][:],
                              in_=w1[:, g * K_PASS:(g + 1) * K_PASS].rearrange("(f p) k -> p f k", p=P))

        for g in range(4):
            load_w(g)

        w_codes = keep.tile([P, PASSES, F], U32, name="w_codes", align_bytes=64)
        w_scales = keep.tile([P, PASSES, F], U8, name="w_scales", align_bytes=64)
        bias = keep.tile([P, F], BF16, name="bias")

        gb_bank = psum_a.tile([P, BANK], F32, name="gb_bank", tag="a")
        nc.tensor.transpose(out=gb_bank[:, 0:P], in_=gb_rows[:].bitcast(F32), identity=ident[:])
        gb = keep.tile([P, P], F32, name="gb")
        nc.vector.tensor_copy(out=gb[:], in_=gb_bank[:].bitcast(BF16)[:, 0:P])
        gamma = gb[:, 0:4 * PASSES]
        beta = gb[:, 64:64 + 4 * PASSES]

        def transpose_h(bank, q, g):
            for u in range(2):
                for bb in range(2):
                    word0 = P * (2 * g + u)
                    nc.tensor.transpose(out=bank[:, ROWS * u + P * bb:ROWS * u + P * bb + P],
                                        in_=h_sb[2 * q + bb][:].bitcast(F32)[:, word0:word0 + P],
                                        identity=ident[:])

        stats = keep.tile([P, PASSES, 2, PAIRS, 8], F32, name="stats")

        def vector_unit(q, g):
            bank = psum_b.tile([P, BANK], F32, name="v_bank", tag="b")
            transpose_h(bank, q, g)
            for u in range(2):
                nc.vector.bn_stats(out=stats[:, g, u, q, 0:6],
                                   in_=bank[:].bitcast(BF16)[:, 2 * ROWS * u:2 * ROWS * (u + 1)])

        def scalar_unit(q, g):
            bank = psum_a.tile([P, BANK], F32, name="s_bank", tag="a")
            transpose_h(bank, q, g)
            x = bank[:].bitcast(BF16).rearrange("p (u r e) -> p u r e", u=2, e=2)
            sums = scalar_stats.tile([P, 4], F32, name="sums", tag="sums")
            for u in range(2):
                for e in range(2):
                    unused = scalar_stats.tile([P, ROWS], BF16, name="unused", tag="unused")
                    nc.scalar.activation(out=unused[:], in_=x[:, u, :, e], func=ACT.Identity,
                                         accum_out=sums[:, 2 * u + e:2 * u + e + 1])
            nc.scalar.activation(out=stats[:, g, :, q, 1:5:3], in_=sums[:].rearrange("p (u e) -> p u e", e=2),
                                 func=ACT.Copy, scale=1.0 / ROWS)
            for u in range(2):
                for e in range(2):
                    unused = scalar_stats.tile([P, ROWS], BF16, name="unused", tag="unused")
                    nc.scalar.activation(out=unused[:], in_=x[:, u, :, e], func=ACT.Square, scale=-1.0,
                                         bias=stats[:, g, u, q, 3 * e + 1:3 * e + 2],
                                         accum_out=stats[:, g, u, q, 3 * e + 2:3 * e + 3])

        w_bf = {}

        def w_group(g):
            w_bf[g] = w_grouped.tile([P, 4 * F], BF16, name="w_bf", tag="w_bf", align_bytes=64)
            grouped = w_bf[g][:].bitcast(F32).rearrange("p (f u) -> p f u", u=2)
            words = w_sb[g][:].bitcast(F32)
            for part in range(4):
                bank = psum_a.tile([P, BANK], F32, name="w_bank", tag="a")
                for u in range(2):
                    for ft in range(2):
                        nc.tensor.transpose(out=bank[:, 2 * P * u + P * ft:2 * P * u + P * ft + P],
                                            in_=words[:, 2 * part + ft, P * u:P * u + P], identity=ident[:])
                nc.scalar.copy(out=grouped[:, 2 * P * part:2 * P * (part + 1), :],
                               in_=bank[:].rearrange("p (u f) -> p f u", u=2))
            if g + 4 < PASSES:
                load_w(g + 4)

        def w_quantise(g):
            nc.vector.quantize_mx(out=w_codes[:, g, :].bitcast(FP8X4), scales=w_scales[:, g, :], in_=w_bf[g][:])

        units = 0
        for q in range(PAIRS):
            for g in range(V_PASSES):
                if g == 2:
                    scalar_unit(q, V_PASSES)
                if g == 6:
                    scalar_unit(q, V_PASSES + 1)
                vector_unit(q, g)
                units += 1
                if units >= W_FIRST_UNIT and units % 2 == 0:
                    w_group((units - W_FIRST_UNIT) // 2)
                    if units > W_FIRST_UNIT:
                        w_quantise((units - W_FIRST_UNIT) // 2 - 1)

        chunk_mean = stats[:, :, :, :, 1:5:3].rearrange("p g u q e -> p (g u) e q")
        chunk_m2 = stats[:, :, :, :, 2:6:3].rearrange("p g u q e -> p (g u) e q")
        shape3 = [P, 2 * PASSES, 2]
        mean_sum = keep.tile(shape3, F32, name="mean_sum")
        mean = keep.tile(shape3, F32, name="mean")
        m2_sum = keep.tile(shape3, F32, name="m2_sum")
        dist = keep.tile(shape3 + [PAIRS], F32, name="dist")
        dist2 = keep.tile(shape3 + [PAIRS], F32, name="dist2")
        dist2_sum = keep.tile(shape3, F32, name="dist2_sum")
        flat = [P, 4 * PASSES]
        within = keep.tile(flat, F32, name="within")
        var_eps = keep.tile(flat, F32, name="var_eps")
        root = keep.tile(flat, F32, name="root")
        inv_root = keep.tile(flat, F32, name="inv_root")
        quotient = keep.tile(flat, F32, name="quotient")
        two_roots = keep.tile(flat, F32, name="two_roots")
        inv_two_roots = keep.tile(flat, F32, name="inv_two_roots")
        scale = keep.tile(flat, F32, name="scale")
        mean_scaled = keep.tile(flat, F32, name="mean_scaled")
        offset = keep.tile(flat, F32, name="offset")
        nc.vector.tensor_reduce(out=mean_sum[:], in_=chunk_mean, axis=AXIS_X, op=ALU.add)
        nc.vector.tensor_reduce(out=m2_sum[:], in_=chunk_m2, axis=AXIS_X, op=ALU.add)
        nc.vector.tensor_scalar_mul(out=mean[:], in0=mean_sum[:], scalar1=1.0 / PAIRS)
        nc.vector.tensor_scalar(out=within[:], in0=m2_sum[:].rearrange("p j e -> p (j e)"), scalar1=1.0 / B,
                                scalar2=EPS, op0=ALU.mult, op1=ALU.add)
        nc.vector.tensor_tensor(out=dist[:], in0=chunk_mean,
                                in1=mean[:].unsqueeze(3).to_broadcast(shape3 + [PAIRS]), op=ALU.subtract)
        nc.vector.tensor_tensor(out=dist2[:], in0=dist[:], in1=dist[:], op=ALU.mult)
        nc.vector.tensor_reduce(out=dist2_sum[:], in_=dist2[:], axis=AXIS_X, op=ALU.add)
        nc.vector.scalar_tensor_tensor(out=var_eps[:], in0=dist2_sum[:].rearrange("p j e -> p (j e)"),
                                       scalar=1.0 / PAIRS, in1=within[:], op0=ALU.mult, op1=ALU.add)
        nc.scalar.activation(out=root[:], in_=var_eps[:], func=ACT.Sqrt)
        w_group(W_AHEAD - 1)
        w_quantise(W_AHEAD - 2)

        x_banks = {}
        n_tiles = {}
        c_bf = {}
        c_mx = {}
        acc = {}

        def transposes(d):
            for half in range(2):
                x_banks[(d, half)] = psum_a.tile([P, BANK], F32, name="x_bank", tag="a")
                transpose_h(x_banks[(d, half)], d // 5, 2 * (d % 5) + half)

        def norm(d):
            for half in range(2):
                g = 2 * (d % 5) + half
                x = x_banks[(d, half)][:].bitcast(BF16).rearrange("p (u r e) -> p u r e", u=2, e=2)
                n_tiles[(d, half)] = normed.tile([P, 4, ROWS], F32, name="n_tile", tag="n_tile")
                for u in range(2):
                    for e in range(2):
                        col = 4 * g + 2 * u + e
                        nc.scalar.activation(out=n_tiles[(d, half)][:, 2 * u + e, :], in_=x[:, u, :, e],
                                             func=ACT.Identity, scale=scale[:, col:col + 1],
                                             bias=offset[:, col:col + 1])

        def leaky_relu(d, half):
            if half == 0:
                c_bf[d] = c_tiles.tile([P, 8 * ROWS], BF16, name="c_bf", tag="c_bf", align_bytes=64)
            n = n_tiles[(d, half)][:].rearrange("p t r -> p r t")
            nc.vector.scalar_tensor_tensor(
                out=c_bf[d][:, 4 * ROWS * half:4 * ROWS * (half + 1)].rearrange("p (r t) -> p r t", t=4),
                in0=n, scalar=SLOPE, in1=n, op0=ALU.mult, op1=ALU.max)

        def quantise(d):
            codes = c_tiles.tile([P, 2 * ROWS], U32, name="c_codes", tag="c_codes", align_bytes=64)
            scales = c_tiles.tile([P, 2 * ROWS], U8, name="c_scales", tag="c_scales", align_bytes=64)
            c_mx[d] = (codes, scales)
            nc.vector.quantize_mx(out=codes[:].bitcast(FP8X4), scales=scales[:], in_=c_bf[d][:])

        def mx_passes(d):
            r = d // 5
            if d % 5 == 0:
                acc[r] = [[psum_b.tile([P, BANK], F32, name="acc", tag="b") for fh in range(2)] for bb in range(2)]
            codes, scales = c_mx[d]
            for bb in range(2):
                for fh in range(2):
                    for half in range(2):
                        g = 2 * (d % 5) + half
                        rows = slice(ROWS * half + P * bb, ROWS * half + P * bb + P)
                        outs = slice(BANK * fh, BANK * (fh + 1))
                        nc.tensor.matmul_mx(out=acc[r][bb][fh][:],
                                            lhsT=codes[:, rows].bitcast(FP8X4), lhsT_scale=scales[:, rows],
                                            rhs=w_codes[:, g, outs].bitcast(FP8X4), rhs_scale=w_scales[:, g, outs],
                                            start=(g == 0), stop=(g == PASSES - 1))

        def add_bias_and_store(r):
            for bb in range(2):
                for fh in range(2):
                    outs = slice(BANK * fh, BANK * (fh + 1))
                    res = result.tile([P, BANK], F32, name="res", tag="res")
                    nc.vector.tensor_tensor(out=res[:], in0=acc[r][bb][fh][:], in1=bias[:, outs], op=ALU.add)
                    row0 = (2 * r + bb) * P
                    nc.sync.dma_start(out=out[row0:row0 + P, outs], in_=res[:])

        transposes(0)
        nc.vector.reciprocal(out=inv_root[:], in_=root[:])
        nc.vector.tensor_tensor(out=quotient[:], in0=var_eps[:], in1=inv_root[:], op=ALU.mult)
        nc.vector.tensor_tensor(out=two_roots[:], in0=quotient[:], in1=root[:], op=ALU.add)
        nc.vector.reciprocal(out=inv_two_roots[:], in_=two_roots[:])
        nc.vector.scalar_tensor_tensor(out=scale[:], in0=gamma, scalar=2.0, in1=inv_two_roots[:],
                                       op0=ALU.mult, op1=ALU.mult)
        nc.vector.tensor_tensor(out=mean_scaled[:], in0=mean[:].rearrange("p j e -> p (j e)"), in1=scale[:],
                                op=ALU.mult)
        nc.vector.tensor_tensor(out=offset[:], in0=beta, in1=mean_scaled[:], op=ALU.subtract)
        nc.sync.dma_start(out=bias[:], in_=b1.partition_broadcast(P))

        for p in range(STEPS + 3):
            if p < STEPS:
                norm(p)
            if p + W_AHEAD < PASSES:
                w_group(p + W_AHEAD)
            if p + 1 < STEPS:
                transposes(p + 1)
            if 1 <= p <= STEPS:
                leaky_relu(p - 1, 0)
            if p >= 7 and (p - 7) % 5 == 0:
                add_bias_and_store((p - 7) // 5)
            if 2 <= p <= STEPS + 1:
                quantise(p - 2)
            if 1 <= p <= STEPS:
                leaky_relu(p - 1, 1)
            if p + W_AHEAD - 1 < PASSES:
                w_quantise(p + W_AHEAD - 1)
            if 2 <= p <= STEPS + 1:
                mx_passes(p - 2)
